import numpy as np
import ml_dtypes


def mxq(x, axis, fmt="e4m3"):
    dtype, down = {"e4m3": (ml_dtypes.float8_e4m3fn, 7), "e5m2": (ml_dtypes.float8_e5m2, 14)}[fmt]
    v = np.moveaxis(np.asarray(x, np.float32).astype(ml_dtypes.bfloat16).astype(np.float64), axis, -1)
    blocks = v.reshape(v.shape[:-1] + (-1, 32))
    amax = np.abs(blocks).max(-1, keepdims=True)
    byte = np.maximum(np.where(amax > 0, np.frexp(amax)[1] - 1 + 127, 0) - down, 1)
    scale = np.exp2(byte - 127.0)
    codes = (blocks / scale).astype(np.float32).astype(dtype).astype(np.float64)
    return np.moveaxis((codes * scale).reshape(v.shape), -1, axis)


WIDE = False


def mx_kscale(k):
    if not WIDE:
        return np.ones(k)
    levels = np.array([10, -10, 5, -5, 0])
    a = np.random.permutation(np.resize(levels, k // 512 * 4)).reshape(k // 512, 4)
    idx = np.arange(k)
    return np.exp2(a[idx // 512, idx % 128 // 32])


BF16 = ml_dtypes.bfloat16


def bf(x):
    return np.asarray(x, np.float32).astype(BF16)


def f64(x):
    return np.asarray(x).astype(np.float64)


E2M1 = np.array([0.0, 0.5, 1.0, 1.5, 2.0, 3.0, 4.0, 6.0, -0.0, -0.5, -1.0, -1.5, -2.0, -3.0, -4.0, -6.0])


def pack_weight(w, fmt):
    k, n = w.shape
    w = f64(bf(w)).reshape(k // 32, 32, n)
    amax = np.abs(w).max(1)
    if fmt == "e4m3":
        byte = np.frexp(amax)[1] - 1 + 127 - 7
    else:
        mant, ex = np.frexp(amax / 6.0)
        byte = np.where(mant > 0.5, ex, ex - 1) + 127
    byte = np.clip(np.where(amax > 0, byte, 1), 1, 254)
    scaled = (w * np.exp2(127.0 - byte)[:, None, :]).reshape(k, n).astype(np.float32)
    by_word = np.ascontiguousarray(scaled.reshape(k // 512, 128, 4, n).transpose(0, 1, 3, 2))
    if fmt == "e4m3":
        words = by_word.astype(ml_dtypes.float8_e4m3fn).view(np.uint8)
    else:
        c = by_word.astype(ml_dtypes.float4_e2m1fn).view(np.uint8) & 0xF
        words = c[..., 0::2] | (c[..., 1::2] << 4)
    return np.ascontiguousarray(words), np.ascontiguousarray(byte.astype(np.uint8).reshape(k // 512, 16, n))


def unpack_weight(words, scales, fmt):
    g, p, n, _ = words.shape
    if fmt == "e4m3":
        vals = np.ascontiguousarray(words).view(ml_dtypes.float8_e4m3fn).astype(np.float64)
    else:
        nib = np.empty((g, p, n, 4), np.uint8)
        nib[..., 0::2] = words & 0xF
        nib[..., 1::2] = words >> 4
        vals = E2M1[nib]
    vals = vals * np.repeat(np.exp2(scales.astype(np.float64) - 127.0), 8, axis=1)[..., None]
    return vals.transpose(0, 1, 3, 2).reshape(g * 512, n)

def pack4(w):
    words, scales = pack_weight(w, "e2m1")
    return words.reshape(words.shape[0], 128, -1), scales


def unpack4(words, scales):
    return unpack_weight(words.reshape(words.shape[0], 128, -1, 2), scales, "e2m1")


B, CIN, P, COUT, W, H, HEADS = 2, 16384, 512, 1024, 16, 8, 4
N = W * H
EPS = 1e-5


def bn(y, g, b, m, v):
    return (y - f64(m)[None, :, None]) * (f64(g) / np.sqrt(f64(v) + EPS))[None, :, None] + f64(b)[None, :, None]


def setup_inputs():
    s, t = mx_kscale(P), mx_kscale(CIN)
    inp = {}
    inp["h_attn"] = bf(np.maximum(np.random.standard_normal((B, P, N)), 0.0) * s[None, :, None])
    inp["x"] = bf(np.random.standard_normal((B, CIN, N)) * t[None, :, None])
    conv3_w = np.random.standard_normal((COUT, P)) * 1.5 / np.sqrt(P) / s[None, :]
    inp["conv3_w_words"], inp["conv3_w_scales"] = pack4(conv3_w.T)
    inp["bn3_g"] = bf(np.random.uniform(0.5, 1.5, COUT))
    inp["bn3_b"] = bf(np.random.standard_normal(COUT) * 0.3)
    inp["bn3_m"] = bf(np.random.standard_normal(COUT) * 0.3)
    inp["bn3_v"] = bf(np.random.uniform(0.5, 1.5, COUT))
    sc_w = np.random.standard_normal((COUT, CIN)) / np.sqrt(CIN) / t[None, :]
    inp["sc_w_words"], inp["sc_w_scales"] = pack4(sc_w.T)
    inp["sc_b"] = bf(np.random.standard_normal(COUT) * 0.3)
    inp["scbn_g"] = bf(np.random.uniform(0.5, 1.5, COUT))
    inp["scbn_b"] = bf(np.random.standard_normal(COUT) * 0.3)
    inp["scbn_m"] = bf(np.random.standard_normal(COUT) * 0.3)
    inp["scbn_v"] = bf(np.random.uniform(0.5, 1.5, COUT))
    return inp


def reference(h_attn, x, conv3_w_words, conv3_w_scales, bn3_g, bn3_b, bn3_m, bn3_v, sc_w_words, sc_w_scales, sc_b, scbn_g, scbn_b, scbn_m, scbn_v):
    main = bn(unpack4(conv3_w_words, conv3_w_scales).T @ mxq(f64(h_attn), 1, "e4m3"), bn3_g, bn3_b, bn3_m, bn3_v)
    short = (unpack4(sc_w_words, sc_w_scales).T @ mxq(f64(x), 1, "e4m3")) + f64(sc_b)[None, :, None]
    short = bn(short, scbn_g, scbn_b, scbn_m, scbn_v)
    return np.maximum(main + short, 0.0)

@@ -1,0 +1,300 @@
+from contextlib import ExitStack
+
+import concourse.mybir as mybir
+from concourse.masks import make_identity
+
+F32 = mybir.dt.float32
+BF16 = mybir.dt.bfloat16
+I32 = mybir.dt.int32
+U32 = mybir.dt.uint32
+U8 = mybir.dt.uint8
+FP8X4 = mybir.dt.float8_e4m3fn_x4
+FP4X4 = mybir.dt.float4_e2m1fn_x4
+ALU = mybir.AluOpType
+ACT = mybir.ActivationFunctionType
+
+P = 128
+PACK = 4
+K_PASS = P * PACK
+BATCH = 2
+POS = 128
+C_MID = 512
+C_IN = 16384
+C_OUT = 1024
+EPS = 1e-5
+
+N_TILE = 512
+HALVES = C_OUT // N_TILE
+BLOCKS = N_TILE // P
+CH_TILES = C_OUT // P
+GROUPS = C_IN // K_PASS
+CHUNK = 4
+CHUNKS = GROUPS // CHUNK
+QUADRANTS = 4
+ROWS = 4
+PLANE_GROUPS = 16
+PLANE_TILES = GROUPS // PLANE_GROUPS
+BURST = 6
+TRICKLE = 2
+AHEAD = 2
+
+FLOPS = 2 * BATCH * C_OUT * (C_IN + C_MID) * POS
+
+
+def tile_bottleneck_transformer_pb_k_kernel(
+    tc,
+    h_attn,
+    x,
+    conv3_w_words,
+    conv3_w_scales,
+    bn3_g,
+    bn3_b,
+    bn3_m,
+    bn3_v,
+    sc_w_words,
+    sc_w_scales,
+    sc_b,
+    scbn_g,
+    scbn_b,
+    scbn_m,
+    scbn_v,
+    out,
+):
+    nc = tc.nc
+    with ExitStack() as ctx:
+        ctx.enter_context(tc.manual_schedule())
+        keep = ctx.enter_context(tc.tile_pool(name="keep", bufs=1))
+        stage = ctx.enter_context(tc.tile_pool(name="stage", bufs=4))
+        quant = ctx.enter_context(tc.tile_pool(name="quant", bufs=BATCH * (AHEAD + 1) + 1))
+        sums = ctx.enter_context(tc.psum_pool(name="sums", bufs=1))
+        work = ctx.enter_context(tc.psum_pool(name="work", bufs=4))
+
+        x_raw = [
+            [keep.tile([P, CHUNK, PACK, POS], BF16, name="x_raw_%d_%d" % (c, b)) for b in range(BATCH)]
+            for c in range(CHUNKS)
+        ]
+        sc_words = [
+            keep.tile([P, CHUNK, 2 * C_OUT], U8, name="sc_words_%d" % c, align_bytes=64) for c in range(CHUNKS)
+        ]
+        sc_planes = [
+            keep.tile([P, PLANE_GROUPS, C_OUT], U8, name="sc_planes_%d" % i, align_bytes=64)
+            for i in range(PLANE_TILES)
+        ]
+        h_raw = keep.tile([P, BATCH, PACK, POS], BF16)
+        c3_words = keep.tile([P, 2 * C_OUT], U8, align_bytes=64)
+        c3_plane = keep.tile([P, C_OUT], U8, align_bytes=64)
+        vec_rows = keep.tile([P, P], BF16)
+        ident = keep.tile([P, P], F32)
+        main_part = keep.tile([P, BATCH, CH_TILES, POS], F32)
+
+        nc.vector.memset(vec_rows[:], 0.0)
+        nc.vector.memset(c3_plane[:].bitcast(I32), 0)
+        for plane in sc_planes:
+            nc.vector.memset(plane[:].bitcast(I32), 0)
+
+        vectors = (bn3_v, scbn_v, bn3_g, scbn_g, bn3_m, scbn_m, bn3_b, scbn_b, sc_b)
+        for v, vec in enumerate(vectors):
+            nc.gpsimd.dma_start(
+                out=vec_rows[CH_TILES * v : CH_TILES * (v + 1), :], in_=vec.rearrange("(c i) -> c i", i=P)
+            )
+        make_identity(nc, ident[:])
+
+        sc_scales_i32 = sc_w_scales.bitcast(I32)
+        sc_words_i32 = sc_w_words.bitcast(I32)
+
+        scale_rows = [(r, quadrant) for r in range(ROWS) for quadrant in (0, 2, 1, 3)]
+
+        def load_scale_rows(i, first, count):
+            for r, quadrant in scale_rows[first : first + count]:
+                partition = 32 * quadrant + r
+                q = ROWS * quadrant + r
+                nc.sync.dma_start(
+                    out=sc_planes[i][:].bitcast(I32)[partition : partition + 1, :, :],
+                    in_=sc_scales_i32[PLANE_GROUPS * i : PLANE_GROUPS * (i + 1), q : q + 1, :].rearrange(
+                        "g o n -> o g n"
+                    ),
+                )
+
+        def load_scale_rows_after(turn):
+            burst_turns = -(-len(scale_rows) // BURST)
+            load_scale_rows(0, BURST * turn, BURST)
+            if turn >= burst_turns:
+                load_scale_rows(1, TRICKLE * (turn - burst_turns), TRICKLE)
+
+        for c in range(CHUNKS):
+            for b in range(BATCH):
+                rows = x[b, CHUNK * K_PASS * c : CHUNK * K_PASS * (c + 1), :]
+                nc.sync.dma_start(out=x_raw[c][b][:], in_=rows.rearrange("(g p t) w -> p g t w", p=P, t=PACK))
+                load_scale_rows_after(3 * c + b)
+            nc.sync.dma_start(
+                out=sc_words[c][:].bitcast(I32),
+                in_=sc_words_i32[CHUNK * c : CHUNK * (c + 1)].rearrange("g p n -> p g n"),
+            )
+            load_scale_rows_after(3 * c + 2)
+            if c == 0:
+                nc.sync.dma_start(out=h_raw[:], in_=h_attn.rearrange("b (p t) w -> p b t w", t=PACK))
+                nc.sync.dma_start(out=c3_words[:].bitcast(I32), in_=conv3_w_words[0].bitcast(I32))
+                for quadrant in range(QUADRANTS):
+                    nc.sync.dma_start(
+                        out=c3_plane[32 * quadrant : 32 * quadrant + ROWS, :].bitcast(I32),
+                        in_=conv3_w_scales[0, ROWS * quadrant : ROWS * (quadrant + 1), :].bitcast(I32),
+                    )
+
+        def quantise(raw, blocks, copy):
+            grouped = stage.tile([P, blocks, POS, PACK], BF16, tag="grouped", align_bytes=64)
+            copy(out=grouped[:], in_=raw[:].rearrange("p g t w -> p g w t"))
+            codes = quant.tile([P, blocks * POS], U32, tag="codes", align_bytes=64)
+            scales = quant.tile([P, blocks * POS], U8, tag="scales", align_bytes=64)
+            nc.vector.quantize_mx(
+                out=codes[:].bitcast(FP8X4), scales=scales[:], in_=grouped[:].rearrange("p g w t -> p (g w t)")
+            )
+            return codes, scales
+
+        x_q = {}
+
+        def quantise_chunk(c):
+            x_q[(c, 0)] = quantise(x_raw[c][0], CHUNK, nc.vector.tensor_copy)
+            x_q[(c, 1)] = quantise(x_raw[c][1], CHUNK, nc.scalar.copy)
+
+        short_sum = [
+            [sums.tile([P, N_TILE], F32, name="short_sum_%d_%d" % (b, h)) for h in range(HALVES)]
+            for b in range(BATCH)
+        ]
+
+        def short_passes(c):
+            for i in range(CHUNK):
+                g = CHUNK * c + i
+                for b in range(BATCH):
+                    codes, scales = x_q[(c, b)]
+                    for h in range(HALVES):
+                        nc.tensor.matmul_mx(
+                            out=short_sum[b][h][:],
+                            lhsT=codes[:, POS * i : POS * (i + 1)].bitcast(FP8X4),
+                            lhsT_scale=scales[:, POS * i : POS * (i + 1)],
+                            rhs=sc_words[c][:, i, 2 * N_TILE * h : 2 * N_TILE * (h + 1)].bitcast(FP4X4),
+                            rhs_scale=sc_planes[g // PLANE_GROUPS][
+                                :, g % PLANE_GROUPS, N_TILE * h : N_TILE * (h + 1)
+                            ],
+                            start=(g == 0),
+                            stop=(g == GROUPS - 1),
+                        )
+
+        banks = [(b, h) for b in range(BATCH) for h in range(HALVES)]
+
+        def copy_out(n, bank):
+            by_position = stage.tile([P, N_TILE], F32, tag="by_position")
+            if n % 2 == 0:
+                nc.vector.tensor_copy(out=by_position[:], in_=bank[:])
+            else:
+                nc.scalar.copy(out=by_position[:], in_=bank[:])
+            return by_position
+
+        def transpose_bank(by_position):
+            by_channel = work.tile([P, BLOCKS, POS], F32, tag="work")
+            for j in range(BLOCKS):
+                nc.tensor.transpose(by_channel[:, j, :], by_position[:, P * j : P * (j + 1)], ident[:])
+            return by_channel
+
+        main_state = {}
+
+        def main_passes():
+            codes, scales = quantise(h_raw, BATCH, nc.scalar.copy)
+            for b, h in banks:
+                main_sum = work.tile([P, N_TILE], F32, tag="work")
+                nc.tensor.matmul_mx(
+                    out=main_sum[:],
+                    lhsT=codes[:, POS * b : POS * (b + 1)].bitcast(FP8X4),
+                    lhsT_scale=scales[:, POS * b : POS * (b + 1)],
+                    rhs=c3_words[:, 2 * N_TILE * h : 2 * N_TILE * (h + 1)].bitcast(FP4X4),
+                    rhs_scale=c3_plane[:, N_TILE * h : N_TILE * (h + 1)],
+                    start=True,
+                    stop=True,
+                )
+                main_state[("sum", b, h)] = main_sum
+
+        def main_copies_and_vector_transpose():
+            for n, (b, h) in enumerate(banks):
+                main_state[("by_position", b, h)] = copy_out(n, main_state[("sum", b, h)])
+            vec_rows_f32 = keep.tile([P, P], F32)
+            nc.vector.tensor_copy(out=vec_rows_f32[:], in_=vec_rows[:])
+            vec_ps = work.tile([P, P], F32, tag="work")
+            nc.tensor.transpose(vec_ps[:], vec_rows_f32[:], ident[:])
+            main_state["vec_ps"] = vec_ps
+
+        def main_transposes_and_gains():
+            cols = keep.tile([P, len(vectors), CH_TILES], F32)
+            nc.vector.tensor_copy(
+                out=cols[:].rearrange("p v c -> p (v c)"), in_=main_state["vec_ps"][:, 0 : len(vectors) * CH_TILES]
+            )
+            for b, h in banks:
+                main_state[("by_channel", b, h)] = transpose_bank(main_state[("by_position", b, h)])
+            gain = keep.tile([P, 2, CH_TILES], F32)
+            nc.vector.tensor_scalar_add(gain[:], cols[:, 0:2, :], EPS)
+            nc.scalar.sqrt(gain[:], gain[:])
+            nc.vector.reciprocal(gain[:], gain[:])
+            nc.vector.tensor_mul(gain[:], gain[:], cols[:, 2:4, :])
+            mean_gain = keep.tile([P, 2, CH_TILES], F32)
+            nc.vector.tensor_mul(mean_gain[:], cols[:, 4:6, :], gain[:])
+            shift = keep.tile([P, CH_TILES], F32)
+            nc.vector.tensor_mul(shift[:], cols[:, 8, :], gain[:, 1, :])
+            nc.vector.tensor_add(shift[:], shift[:], cols[:, 6, :])
+            nc.vector.tensor_add(shift[:], shift[:], cols[:, 7, :])
+            nc.vector.tensor_sub(shift[:], shift[:], mean_gain[:, 0, :])
+            nc.vector.tensor_sub(shift[:], shift[:], mean_gain[:, 1, :])
+            main_state["gain"] = gain
+            main_state["shift"] = shift
+
+        def main_scale_and_shift():
+            gain, shift = main_state["gain"], main_state["shift"]
+            for n, (b, h) in enumerate(banks):
+                by_channel = main_state[("by_channel", b, h)]
+                for j in range(BLOCKS):
+                    c = BLOCKS * h + j
+                    if n % 2 == 0:
+                        nc.vector.tensor_scalar(
+                            out=main_part[:, b, c, :],
+                            in0=by_channel[:, j, :],
+                            scalar1=gain[:, 0, c : c + 1],
+                            scalar2=shift[:, c : c + 1],
+                            op0=ALU.mult,
+                            op1=ALU.add,
+                        )
+                    else:
+                        nc.scalar.activation(
+                            out=main_part[:, b, c, :],
+                            in_=by_channel[:, j, :],
+                            func=ACT.Identity,
+                            scale=gain[:, 0, c : c + 1],
+                            bias=shift[:, c : c + 1],
+                        )
+
+        main_steps = (main_passes, main_copies_and_vector_transpose, main_transposes_and_gains, main_scale_and_shift)
+
+        for c in range(AHEAD):
+            quantise_chunk(c)
+        for c in range(CHUNKS):
+            short_passes(c)
+            if c + AHEAD < CHUNKS:
+                quantise_chunk(c + AHEAD)
+            if c < len(main_steps):
+                main_steps[c]()
+
+        gain = main_state["gain"]
+        short_by_position = [copy_out(n, short_sum[b][h]) for n, (b, h) in enumerate(banks)]
+        for n, (b, h) in enumerate(banks):
+            by_channel = transpose_bank(short_by_position[n])
+            result = stage.tile([P, BLOCKS, POS], F32, tag="result")
+            for j in range(BLOCKS):
+                c = BLOCKS * h + j
+                nc.vector.scalar_tensor_tensor(
+                    out=result[:, j, :],
+                    in0=by_channel[:, j, :],
+                    scalar=gain[:, 1, c : c + 1],
+                    in1=main_part[:, b, c, :],
+                    op0=ALU.mult,
+                    op1=ALU.add,
+                )
+            nc.scalar.activation(out=result[:], in_=result[:], func=ACT.Relu)
+            nc.sync.dma_start(
+                out=out[b, N_TILE * h : N_TILE * (h + 1), :].rearrange("(j p) w -> p j w", p=P), in_=result[:]
+            )

@@ -25,18 +25,18 @@ EPS = 1e-5
 
 N_TILE = 512
 HALVES = C_OUT // N_TILE
-BLOCKS = N_TILE // P
-CH_TILES = C_OUT // P
+PER_ROW = C_OUT // P
+HALF_P = N_TILE // PER_ROW
+BLOCKS = N_TILE // POS
 GROUPS = C_IN // K_PASS
-CHUNK = 4
+CHUNK = 2
 CHUNKS = GROUPS // CHUNK
 QUADRANTS = 4
 ROWS = 4
 PLANE_GROUPS = 16
 PLANE_TILES = GROUPS // PLANE_GROUPS
 BURST = 6
-TRICKLE = 2
-AHEAD = 2
+TRICKLE = 1
 
 FLOPS = 2 * BATCH * C_OUT * (C_IN + C_MID) * POS
 
@@ -65,7 +65,8 @@ def tile_bottleneck_transformer_pb_k_kernel(
         ctx.enter_context(tc.manual_schedule())
         keep = ctx.enter_context(tc.tile_pool(name="keep", bufs=1))
         stage = ctx.enter_context(tc.tile_pool(name="stage", bufs=4))
-        quant = ctx.enter_context(tc.tile_pool(name="quant", bufs=BATCH * (AHEAD + 1) + 1))
+        wide = ctx.enter_context(tc.tile_pool(name="wide", bufs=BATCH))
+        quant = ctx.enter_context(tc.tile_pool(name="quant", bufs=3 * BATCH + 1))
         sums = ctx.enter_context(tc.psum_pool(name="sums", bufs=1))
         work = ctx.enter_context(tc.psum_pool(name="work", bufs=4))
 
@@ -83,21 +84,41 @@ def tile_bottleneck_transformer_pb_k_kernel(
         h_raw = keep.tile([P, BATCH, PACK, POS], BF16)
         c3_words = keep.tile([P, 2 * C_OUT], U8, align_bytes=64)
         c3_plane = keep.tile([P, C_OUT], U8, align_bytes=64)
-        vec_rows = keep.tile([P, P], BF16)
         ident = keep.tile([P, P], F32)
-        main_part = keep.tile([P, BATCH, CH_TILES, POS], F32)
+        main_part = keep.tile([P, BATCH, PER_ROW, POS], F32)
 
-        nc.vector.memset(vec_rows[:], 0.0)
         nc.vector.memset(c3_plane[:].bitcast(I32), 0)
         for plane in sc_planes:
             nc.vector.memset(plane[:].bitcast(I32), 0)
 
         vectors = (bn3_v, scbn_v, bn3_g, scbn_g, bn3_m, scbn_m, bn3_b, scbn_b, sc_b)
+        slots = keep.tile([P, len(vectors), 2 * PER_ROW], BF16)
         for v, vec in enumerate(vectors):
-            nc.gpsimd.dma_start(
-                out=vec_rows[CH_TILES * v : CH_TILES * (v + 1), :], in_=vec.rearrange("(c i) -> c i", i=P)
-            )
+            nc.gpsimd.dma_start(out=slots[:, v, 0:PER_ROW], in_=vec.rearrange("(p j) -> p j", j=PER_ROW))
         make_identity(nc, ident[:])
+        variance, weight, mean = [slots[:, 2 * i : 2 * i + 2, 0:PER_ROW] for i in range(3)]
+        minus_half = keep.tile([P, 2, PER_ROW], F32)
+        nc.gpsimd.memset(minus_half[:], -0.5)
+        gain = keep.tile([P, 2, PER_ROW], F32)
+        nc.gpsimd.tensor_scalar_add(gain[:], variance, EPS)
+        nc.gpsimd.tensor_tensor(out=gain[:], in0=gain[:], in1=minus_half[:], op=ALU.pow)
+        nc.gpsimd.tensor_tensor(out=gain[:], in0=gain[:], in1=weight, op=ALU.mult)
+        mean_gain = keep.tile([P, 2, PER_ROW], F32)
+        nc.gpsimd.tensor_tensor(out=mean_gain[:], in0=gain[:], in1=mean, op=ALU.mult)
+        shift = keep.tile([P, PER_ROW], F32)
+        nc.gpsimd.tensor_tensor(out=shift[:], in0=gain[:, 1, :], in1=slots[:, 8, 0:PER_ROW], op=ALU.mult)
+        nc.gpsimd.tensor_tensor(out=shift[:], in0=shift[:], in1=slots[:, 6, 0:PER_ROW], op=ALU.add)
+        nc.gpsimd.tensor_tensor(out=shift[:], in0=shift[:], in1=slots[:, 7, 0:PER_ROW], op=ALU.add)
+        nc.gpsimd.tensor_tensor(out=shift[:], in0=shift[:], in1=mean_gain[:, 0, :], op=ALU.subtract)
+        nc.gpsimd.tensor_tensor(out=shift[:], in0=shift[:], in1=mean_gain[:, 1, :], op=ALU.subtract)
+
+        nc.sync.dma_start(out=h_raw[:], in_=h_attn.rearrange("b (p t) w -> p b t w", t=PACK))
+        nc.sync.dma_start(out=c3_words[:].bitcast(I32), in_=conv3_w_words[0].bitcast(I32))
+        for quadrant in range(QUADRANTS):
+            nc.sync.dma_start(
+                out=c3_plane[32 * quadrant : 32 * quadrant + ROWS, :].bitcast(I32),
+                in_=conv3_w_scales[0, ROWS * quadrant : ROWS * (quadrant + 1), :].bitcast(I32),
+            )
 
         sc_scales_i32 = sc_w_scales.bitcast(I32)
         sc_words_i32 = sc_w_words.bitcast(I32)
@@ -131,14 +152,6 @@ def tile_bottleneck_transformer_pb_k_kernel(
                 in_=sc_words_i32[CHUNK * c : CHUNK * (c + 1)].rearrange("g p n -> p g n"),
             )
             load_scale_rows_after(3 * c + 2)
-            if c == 0:
-                nc.sync.dma_start(out=h_raw[:], in_=h_attn.rearrange("b (p t) w -> p b t w", t=PACK))
-                nc.sync.dma_start(out=c3_words[:].bitcast(I32), in_=conv3_w_words[0].bitcast(I32))
-                for quadrant in range(QUADRANTS):
-                    nc.sync.dma_start(
-                        out=c3_plane[32 * quadrant : 32 * quadrant + ROWS, :].bitcast(I32),
-                        in_=conv3_w_scales[0, ROWS * quadrant : ROWS * (quadrant + 1), :].bitcast(I32),
-                    )
 
         def quantise(raw, blocks, copy):
             grouped = stage.tile([P, blocks, POS, PACK], BF16, tag="grouped", align_bytes=64)
@@ -162,10 +175,10 @@ def tile_bottleneck_transformer_pb_k_kernel(
         ]
 
         def short_passes(c):
-            for i in range(CHUNK):
-                g = CHUNK * c + i
-                for b in range(BATCH):
-                    codes, scales = x_q[(c, b)]
+            for b in range(BATCH):
+                codes, scales = x_q[(c, b)]
+                for i in range(CHUNK):
+                    g = CHUNK * c + i
                     for h in range(HALVES):
                         nc.tensor.matmul_mx(
                             out=short_sum[b][h][:],
@@ -179,122 +192,89 @@ def tile_bottleneck_transformer_pb_k_kernel(
                             stop=(g == GROUPS - 1),
                         )
 
-        banks = [(b, h) for b in range(BATCH) for h in range(HALVES)]
+        def main_passes(codes, scales):
+            main_sum = [[work.tile([P, N_TILE], F32, tag="work", name="main_sum") for h in range(HALVES)] for b in range(BATCH)]
+            for b in range(BATCH):
+                for h in range(HALVES):
+                    nc.tensor.matmul_mx(
+                        out=main_sum[b][h][:],
+                        lhsT=codes[:, POS * b : POS * (b + 1)].bitcast(FP8X4),
+                        lhsT_scale=scales[:, POS * b : POS * (b + 1)],
+                        rhs=c3_words[:, 2 * N_TILE * h : 2 * N_TILE * (h + 1)].bitcast(FP4X4),
+                        rhs_scale=c3_plane[:, N_TILE * h : N_TILE * (h + 1)],
+                        start=True,
+                        stop=True,
+                    )
+            return main_sum
 
-        def copy_out(n, bank):
-            by_position = stage.tile([P, N_TILE], F32, tag="by_position")
-            if n % 2 == 0:
-                nc.vector.tensor_copy(out=by_position[:], in_=bank[:])
-            else:
-                nc.scalar.copy(out=by_position[:], in_=bank[:])
+        def copy_out(halves):
+            by_position = wide.tile([P, PER_ROW, P], F32, tag="by_position")
+            for h, copy in enumerate((nc.vector.tensor_copy, nc.scalar.copy)):
+                copy(
+                    out=by_position[:, :, HALF_P * h : HALF_P * (h + 1)],
+                    in_=halves[h][:].rearrange("q (p j) -> q j p", j=PER_ROW),
+                )
             return by_position
 
-        def transpose_bank(by_position):
+        def transpose_blocks(by_position, first):
             by_channel = work.tile([P, BLOCKS, POS], F32, tag="work")
             for j in range(BLOCKS):
-                nc.tensor.transpose(by_channel[:, j, :], by_position[:, P * j : P * (j + 1)], ident[:])
+                nc.tensor.transpose(by_channel[:, j, :], by_position[:, first + j, :], ident[:])
             return by_channel
 
-        main_state = {}
+        units = [(b, first) for b in range(BATCH) for first in range(0, PER_ROW, BLOCKS)]
 
-        def main_passes():
-            codes, scales = quantise(h_raw, BATCH, nc.scalar.copy)
-            for b, h in banks:
-                main_sum = work.tile([P, N_TILE], F32, tag="work")
-                nc.tensor.matmul_mx(
-                    out=main_sum[:],
-                    lhsT=codes[:, POS * b : POS * (b + 1)].bitcast(FP8X4),
-                    lhsT_scale=scales[:, POS * b : POS * (b + 1)],
-                    rhs=c3_words[:, 2 * N_TILE * h : 2 * N_TILE * (h + 1)].bitcast(FP4X4),
-                    rhs_scale=c3_plane[:, N_TILE * h : N_TILE * (h + 1)],
-                    start=True,
-                    stop=True,
-                )
-                main_state[("sum", b, h)] = main_sum
-
-        def main_copies_and_vector_transpose():
-            for n, (b, h) in enumerate(banks):
-                main_state[("by_position", b, h)] = copy_out(n, main_state[("sum", b, h)])
-            vec_rows_f32 = keep.tile([P, P], F32)
-            nc.vector.tensor_copy(out=vec_rows_f32[:], in_=vec_rows[:])
-            vec_ps = work.tile([P, P], F32, tag="work")
-            nc.tensor.transpose(vec_ps[:], vec_rows_f32[:], ident[:])
-            main_state["vec_ps"] = vec_ps
-
-        def main_transposes_and_gains():
-            cols = keep.tile([P, len(vectors), CH_TILES], F32)
-            nc.vector.tensor_copy(
-                out=cols[:].rearrange("p v c -> p (v c)"), in_=main_state["vec_ps"][:, 0 : len(vectors) * CH_TILES]
-            )
-            for b, h in banks:
-                main_state[("by_channel", b, h)] = transpose_bank(main_state[("by_position", b, h)])
-            gain = keep.tile([P, 2, CH_TILES], F32)
-            nc.vector.tensor_scalar_add(gain[:], cols[:, 0:2, :], EPS)
-            nc.scalar.sqrt(gain[:], gain[:])
-            nc.vector.reciprocal(gain[:], gain[:])
-            nc.vector.tensor_mul(gain[:], gain[:], cols[:, 2:4, :])
-            mean_gain = keep.tile([P, 2, CH_TILES], F32)
-            nc.vector.tensor_mul(mean_gain[:], cols[:, 4:6, :], gain[:])
-            shift = keep.tile([P, CH_TILES], F32)
-            nc.vector.tensor_mul(shift[:], cols[:, 8, :], gain[:, 1, :])
-            nc.vector.tensor_add(shift[:], shift[:], cols[:, 6, :])
-            nc.vector.tensor_add(shift[:], shift[:], cols[:, 7, :])
-            nc.vector.tensor_sub(shift[:], shift[:], mean_gain[:, 0, :])
-            nc.vector.tensor_sub(shift[:], shift[:], mean_gain[:, 1, :])
-            main_state["gain"] = gain
-            main_state["shift"] = shift
-
-        def main_scale_and_shift():
-            gain, shift = main_state["gain"], main_state["shift"]
-            for n, (b, h) in enumerate(banks):
-                by_channel = main_state[("by_channel", b, h)]
+        def main_scale_and_shift(main_by_channel):
+            for n, (b, first) in enumerate(units):
                 for j in range(BLOCKS):
-                    c = BLOCKS * h + j
+                    row = first + j
                     if n % 2 == 0:
                         nc.vector.tensor_scalar(
-                            out=main_part[:, b, c, :],
-                            in0=by_channel[:, j, :],
-                            scalar1=gain[:, 0, c : c + 1],
-                            scalar2=shift[:, c : c + 1],
+                            out=main_part[:, b, row, :],
+                            in0=main_by_channel[n][:, j, :],
+                            scalar1=gain[:, 0, row : row + 1],
+                            scalar2=shift[:, row : row + 1],
                             op0=ALU.mult,
                             op1=ALU.add,
                         )
                     else:
                         nc.scalar.activation(
-                            out=main_part[:, b, c, :],
-                            in_=by_channel[:, j, :],
+                            out=main_part[:, b, row, :],
+                            in_=main_by_channel[n][:, j, :],
                             func=ACT.Identity,
-                            scale=gain[:, 0, c : c + 1],
-                            bias=shift[:, c : c + 1],
+                            scale=gain[:, 0, row : row + 1],
+                            bias=shift[:, row : row + 1],
                         )
 
-        main_steps = (main_passes, main_copies_and_vector_transpose, main_transposes_and_gains, main_scale_and_shift)
-
-        for c in range(AHEAD):
-            quantise_chunk(c)
+        h_codes, h_scales = quantise(h_raw, BATCH, nc.scalar.copy)
+        quantise_chunk(0)
+        main_sum = main_passes(h_codes, h_scales)
         for c in range(CHUNKS):
             short_passes(c)
-            if c + AHEAD < CHUNKS:
-                quantise_chunk(c + AHEAD)
-            if c < len(main_steps):
-                main_steps[c]()
+            if c == 1:
+                main_by_channel = [transpose_blocks(main_by_position[b], first) for b, first in units]
+            if c + 1 < CHUNKS:
+                quantise_chunk(c + 1)
+            if c == 0:
+                main_by_position = [copy_out(main_sum[b]) for b in range(BATCH)]
+            if c == CHUNKS // 2:
+                main_scale_and_shift(main_by_channel)
 
-        gain = main_state["gain"]
-        short_by_position = [copy_out(n, short_sum[b][h]) for n, (b, h) in enumerate(banks)]
-        for n, (b, h) in enumerate(banks):
-            by_channel = transpose_bank(short_by_position[n])
+        short_by_position = [copy_out(short_sum[b]) for b in range(BATCH)]
+        for b, first in units:
+            by_channel = transpose_blocks(short_by_position[b], first)
             result = stage.tile([P, BLOCKS, POS], F32, tag="result")
             for j in range(BLOCKS):
-                c = BLOCKS * h + j
+                row = first + j
                 nc.vector.scalar_tensor_tensor(
                     out=result[:, j, :],
                     in0=by_channel[:, j, :],
-                    scalar=gain[:, 1, c : c + 1],
-                    in1=main_part[:, b, c, :],
+                    scalar=gain[:, 1, row : row + 1],
+                    in1=main_part[:, b, row, :],
                     op0=ALU.mult,
                     op1=ALU.add,
                 )
             nc.scalar.activation(out=result[:], in_=result[:], func=ACT.Relu)
             nc.sync.dma_start(
-                out=out[b, N_TILE * h : N_TILE * (h + 1), :].rearrange("(j p) w -> p j w", p=P), in_=result[:]
+                out=out[b].rearrange("(p j) w -> p j w", j=PER_ROW)[:, first : first + BLOCKS, :], in_=result[:]
             )

@@ -25,18 +25,17 @@ EPS = 1e-5
 
 N_TILE = 512
 HALVES = C_OUT // N_TILE
-PER_ROW = C_OUT // P
-HALF_P = N_TILE // PER_ROW
-BLOCKS = N_TILE // POS
+BLOCKS = N_TILE // P
 GROUPS = C_IN // K_PASS
-CHUNK = 2
-CHUNKS = GROUPS // CHUNK
+SIZES = (2, 2, 4, 4, 4, 4, 4, 4, 2, 2)
+FIRSTS = (0, 2, 4, 8, 12, 16, 20, 24, 28, 30)
+CHUNKS = len(SIZES)
+LAST = CHUNKS - 1
 QUADRANTS = 4
 ROWS = 4
 PLANE_GROUPS = 16
 PLANE_TILES = GROUPS // PLANE_GROUPS
-BURST = 6
-TRICKLE = 1
+TRICKLE = 2
 
 FLOPS = 2 * BATCH * C_OUT * (C_IN + C_MID) * POS
 
@@ -65,17 +64,21 @@ def tile_bottleneck_transformer_pb_k_kernel(
         ctx.enter_context(tc.manual_schedule())
         keep = ctx.enter_context(tc.tile_pool(name="keep", bufs=1))
         stage = ctx.enter_context(tc.tile_pool(name="stage", bufs=4))
-        wide = ctx.enter_context(tc.tile_pool(name="wide", bufs=BATCH))
+        wide = ctx.enter_context(tc.tile_pool(name="wide", bufs=4))
         quant = ctx.enter_context(tc.tile_pool(name="quant", bufs=3 * BATCH + 1))
         sums = ctx.enter_context(tc.psum_pool(name="sums", bufs=1))
         work = ctx.enter_context(tc.psum_pool(name="work", bufs=4))
 
         x_raw = [
-            [keep.tile([P, CHUNK, PACK, POS], BF16, name="x_raw_%d_%d" % (c, b)) for b in range(BATCH)]
+            [keep.tile([P, SIZES[c], PACK, POS], BF16, name="x_raw_%d_%d" % (c, b)) for b in range(BATCH)]
             for c in range(CHUNKS)
         ]
         sc_words = [
-            keep.tile([P, CHUNK, 2 * C_OUT], U8, name="sc_words_%d" % c, align_bytes=64) for c in range(CHUNKS)
+            [
+                keep.tile([P, SIZES[c], 2 * C_OUT // parts], U8, name="sc_words_%d_%d" % (c, i), align_bytes=64)
+                for i in range(parts)
+            ]
+            for c, parts in enumerate([1] * LAST + [HALVES])
         ]
         sc_planes = [
             keep.tile([P, PLANE_GROUPS, C_OUT], U8, name="sc_planes_%d" % i, align_bytes=64)
@@ -85,40 +88,31 @@ def tile_bottleneck_transformer_pb_k_kernel(
         c3_words = keep.tile([P, 2 * C_OUT], U8, align_bytes=64)
         c3_plane = keep.tile([P, C_OUT], U8, align_bytes=64)
         ident = keep.tile([P, P], F32)
-        main_part = keep.tile([P, BATCH, PER_ROW, POS], F32)
+        main_part = keep.tile([P, HALVES, BATCH, BLOCKS, POS], F32)
 
         nc.vector.memset(c3_plane[:].bitcast(I32), 0)
-        for plane in sc_planes:
-            nc.vector.memset(plane[:].bitcast(I32), 0)
+        nc.vector.memset(sc_planes[0][:].bitcast(I32), 0)
 
         vectors = (bn3_v, scbn_v, bn3_g, scbn_g, bn3_m, scbn_m, bn3_b, scbn_b, sc_b)
-        slots = keep.tile([P, len(vectors), 2 * PER_ROW], BF16)
+        slots = keep.tile([P, len(vectors), HALVES, 2 * BLOCKS], BF16)
         for v, vec in enumerate(vectors):
-            nc.gpsimd.dma_start(out=slots[:, v, 0:PER_ROW], in_=vec.rearrange("(p j) -> p j", j=PER_ROW))
+            nc.gpsimd.dma_start(out=slots[:, v, :, 0:BLOCKS], in_=vec.rearrange("(h p j) -> p h j", h=HALVES, p=P))
         make_identity(nc, ident[:])
-        variance, weight, mean = [slots[:, 2 * i : 2 * i + 2, 0:PER_ROW] for i in range(3)]
-        minus_half = keep.tile([P, 2, PER_ROW], F32)
+        variance, weight, mean = [slots[:, 2 * i : 2 * i + 2, :, 0:BLOCKS] for i in range(3)]
+        minus_half = keep.tile([P, 2, HALVES, BLOCKS], F32)
         nc.gpsimd.memset(minus_half[:], -0.5)
-        gain = keep.tile([P, 2, PER_ROW], F32)
+        gain = keep.tile([P, 2, HALVES, BLOCKS], F32)
         nc.gpsimd.tensor_scalar_add(gain[:], variance, EPS)
         nc.gpsimd.tensor_tensor(out=gain[:], in0=gain[:], in1=minus_half[:], op=ALU.pow)
         nc.gpsimd.tensor_tensor(out=gain[:], in0=gain[:], in1=weight, op=ALU.mult)
-        mean_gain = keep.tile([P, 2, PER_ROW], F32)
+        mean_gain = keep.tile([P, 2, HALVES, BLOCKS], F32)
         nc.gpsimd.tensor_tensor(out=mean_gain[:], in0=gain[:], in1=mean, op=ALU.mult)
-        shift = keep.tile([P, PER_ROW], F32)
-        nc.gpsimd.tensor_tensor(out=shift[:], in0=gain[:, 1, :], in1=slots[:, 8, 0:PER_ROW], op=ALU.mult)
-        nc.gpsimd.tensor_tensor(out=shift[:], in0=shift[:], in1=slots[:, 6, 0:PER_ROW], op=ALU.add)
-        nc.gpsimd.tensor_tensor(out=shift[:], in0=shift[:], in1=slots[:, 7, 0:PER_ROW], op=ALU.add)
-        nc.gpsimd.tensor_tensor(out=shift[:], in0=shift[:], in1=mean_gain[:, 0, :], op=ALU.subtract)
-        nc.gpsimd.tensor_tensor(out=shift[:], in0=shift[:], in1=mean_gain[:, 1, :], op=ALU.subtract)
-
-        nc.sync.dma_start(out=h_raw[:], in_=h_attn.rearrange("b (p t) w -> p b t w", t=PACK))
-        nc.sync.dma_start(out=c3_words[:].bitcast(I32), in_=conv3_w_words[0].bitcast(I32))
-        for quadrant in range(QUADRANTS):
-            nc.sync.dma_start(
-                out=c3_plane[32 * quadrant : 32 * quadrant + ROWS, :].bitcast(I32),
-                in_=conv3_w_scales[0, ROWS * quadrant : ROWS * (quadrant + 1), :].bitcast(I32),
-            )
+        shift = keep.tile([P, HALVES, BLOCKS], F32)
+        nc.gpsimd.tensor_tensor(out=shift[:], in0=gain[:, 1], in1=slots[:, 8, :, 0:BLOCKS], op=ALU.mult)
+        nc.gpsimd.tensor_tensor(out=shift[:], in0=shift[:], in1=slots[:, 6, :, 0:BLOCKS], op=ALU.add)
+        nc.gpsimd.tensor_tensor(out=shift[:], in0=shift[:], in1=slots[:, 7, :, 0:BLOCKS], op=ALU.add)
+        nc.gpsimd.tensor_tensor(out=shift[:], in0=shift[:], in1=mean_gain[:, 0], op=ALU.subtract)
+        nc.gpsimd.tensor_tensor(out=shift[:], in0=shift[:], in1=mean_gain[:, 1], op=ALU.subtract)
 
         sc_scales_i32 = sc_w_scales.bitcast(I32)
         sc_words_i32 = sc_w_words.bitcast(I32)
@@ -136,22 +130,36 @@ def tile_bottleneck_transformer_pb_k_kernel(
                     ),
                 )
 
-        def load_scale_rows_after(turn):
-            burst_turns = -(-len(scale_rows) // BURST)
-            load_scale_rows(0, BURST * turn, BURST)
-            if turn >= burst_turns:
-                load_scale_rows(1, TRICKLE * (turn - burst_turns), TRICKLE)
+        def load_x(c, b):
+            rows = x[b, K_PASS * FIRSTS[c] : K_PASS * (FIRSTS[c] + SIZES[c]), :]
+            nc.sync.dma_start(out=x_raw[c][b][:], in_=rows.rearrange("(g p t) w -> p g t w", p=P, t=PACK))
 
-        for c in range(CHUNKS):
-            for b in range(BATCH):
-                rows = x[b, CHUNK * K_PASS * c : CHUNK * K_PASS * (c + 1), :]
-                nc.sync.dma_start(out=x_raw[c][b][:], in_=rows.rearrange("(g p t) w -> p g t w", p=P, t=PACK))
-                load_scale_rows_after(3 * c + b)
+        def load_words(c, i):
+            words = sc_words_i32[FIRSTS[c] : FIRSTS[c] + SIZES[c]].rearrange("g p n -> p g n")
+            width = words.shape[2] // len(sc_words[c])
+            nc.sync.dma_start(out=sc_words[c][i][:].bitcast(I32), in_=words[:, :, width * i : width * (i + 1)])
+
+        nc.sync.dma_start(out=h_raw[:], in_=h_attn.rearrange("b (p t) w -> p b t w", t=PACK))
+        nc.sync.dma_start(out=c3_words[:].bitcast(I32), in_=conv3_w_words[0].bitcast(I32))
+        for quadrant in range(QUADRANTS):
             nc.sync.dma_start(
-                out=sc_words[c][:].bitcast(I32),
-                in_=sc_words_i32[CHUNK * c : CHUNK * (c + 1)].rearrange("g p n -> p g n"),
+                out=c3_plane[32 * quadrant : 32 * quadrant + ROWS, :].bitcast(I32),
+                in_=conv3_w_scales[0, ROWS * quadrant : ROWS * (quadrant + 1), :].bitcast(I32),
             )
-            load_scale_rows_after(3 * c + 2)
+        for b in range(BATCH):
+            load_x(0, b)
+        load_words(0, 0)
+        load_scale_rows(0, 0, len(scale_rows))
+
+        def load_rest():
+            large = [(load_x, 1, 0), (load_x, 1, 1)]
+            for c in range(1, CHUNKS):
+                if c < LAST:
+                    large += [(load_x, c + 1, 0), (load_x, c + 1, 1)]
+                large += [(load_words, c, i) for i in range(len(sc_words[c]))]
+            for n, (load, c, i) in enumerate(large):
+                load(c, i)
+                load_scale_rows(1, TRICKLE * n, TRICKLE)
 
         def quantise(raw, blocks, copy):
             grouped = stage.tile([P, blocks, POS, PACK], BF16, tag="grouped", align_bytes=64)
@@ -166,38 +174,36 @@ def tile_bottleneck_transformer_pb_k_kernel(
         x_q = {}
 
         def quantise_chunk(c):
-            x_q[(c, 0)] = quantise(x_raw[c][0], CHUNK, nc.vector.tensor_copy)
-            x_q[(c, 1)] = quantise(x_raw[c][1], CHUNK, nc.scalar.copy)
+            x_q[(c, 0)] = quantise(x_raw[c][0], SIZES[c], nc.vector.tensor_copy)
+            x_q[(c, 1)] = quantise(x_raw[c][1], SIZES[c], nc.scalar.copy)
 
         short_sum = [
             [sums.tile([P, N_TILE], F32, name="short_sum_%d_%d" % (b, h)) for h in range(HALVES)]
             for b in range(BATCH)
         ]
 
-        def short_passes(c):
-            for b in range(BATCH):
-                codes, scales = x_q[(c, b)]
-                for i in range(CHUNK):
-                    g = CHUNK * c + i
-                    for h in range(HALVES):
-                        nc.tensor.matmul_mx(
-                            out=short_sum[b][h][:],
-                            lhsT=codes[:, POS * i : POS * (i + 1)].bitcast(FP8X4),
-                            lhsT_scale=scales[:, POS * i : POS * (i + 1)],
-                            rhs=sc_words[c][:, i, 2 * N_TILE * h : 2 * N_TILE * (h + 1)].bitcast(FP4X4),
-                            rhs_scale=sc_planes[g // PLANE_GROUPS][
-                                :, g % PLANE_GROUPS, N_TILE * h : N_TILE * (h + 1)
-                            ],
-                            start=(g == 0),
-                            stop=(g == GROUPS - 1),
-                        )
+        def short_pass(c, b, i, h):
+            codes, scales = x_q[(c, b)]
+            g = FIRSTS[c] + i
+            words = sc_words[c]
+            rhs = words[h][:, i, :] if len(words) > 1 else words[0][:, i, 2 * N_TILE * h : 2 * N_TILE * (h + 1)]
+            nc.tensor.matmul_mx(
+                out=short_sum[b][h][:],
+                lhsT=codes[:, POS * i : POS * (i + 1)].bitcast(FP8X4),
+                lhsT_scale=scales[:, POS * i : POS * (i + 1)],
+                rhs=rhs.bitcast(FP4X4),
+                rhs_scale=sc_planes[g // PLANE_GROUPS][:, g % PLANE_GROUPS, N_TILE * h : N_TILE * (h + 1)],
+                start=(g == 0),
+                stop=(g == GROUPS - 1),
+            )
 
         def main_passes(codes, scales):
-            main_sum = [[work.tile([P, N_TILE], F32, tag="work", name="main_sum") for h in range(HALVES)] for b in range(BATCH)]
+            main_sum = {}
             for b in range(BATCH):
                 for h in range(HALVES):
+                    main_sum[(h, b)] = work.tile([P, N_TILE], F32, tag="work", name="main_sum")
                     nc.tensor.matmul_mx(
-                        out=main_sum[b][h][:],
+                        out=main_sum[(h, b)][:],
                         lhsT=codes[:, POS * b : POS * (b + 1)].bitcast(FP8X4),
                         lhsT_scale=scales[:, POS * b : POS * (b + 1)],
                         rhs=c3_words[:, 2 * N_TILE * h : 2 * N_TILE * (h + 1)].bitcast(FP4X4),
@@ -207,74 +213,85 @@ def tile_bottleneck_transformer_pb_k_kernel(
                     )
             return main_sum
 
-        def copy_out(halves):
-            by_position = wide.tile([P, PER_ROW, P], F32, tag="by_position")
-            for h, copy in enumerate((nc.vector.tensor_copy, nc.scalar.copy)):
-                copy(
-                    out=by_position[:, :, HALF_P * h : HALF_P * (h + 1)],
-                    in_=halves[h][:].rearrange("q (p j) -> q j p", j=PER_ROW),
-                )
+        units = [(h, b) for h in range(HALVES) for b in range(BATCH)]
+
+        def copy_out(bank, b):
+            by_position = wide.tile([P, BLOCKS, P], F32, tag="by_position")
+            copy = nc.vector.tensor_copy if b == 0 else nc.scalar.copy
+            copy(out=by_position[:], in_=bank[:].rearrange("q (p j) -> q j p", j=BLOCKS))
             return by_position
 
-        def transpose_blocks(by_position, first):
+        def transpose_blocks(by_position):
             by_channel = work.tile([P, BLOCKS, POS], F32, tag="work")
             for j in range(BLOCKS):
-                nc.tensor.transpose(by_channel[:, j, :], by_position[:, first + j, :], ident[:])
+                nc.tensor.transpose(by_channel[:, j, :], by_position[:, j, :], ident[:])
             return by_channel
 
-        units = [(b, first) for b in range(BATCH) for first in range(0, PER_ROW, BLOCKS)]
+        def main_scale_and_shift(h, b, by_channel):
+            for j in range(BLOCKS):
+                if b == 0:
+                    nc.vector.tensor_scalar(
+                        out=main_part[:, h, b, j, :],
+                        in0=by_channel[:, j, :],
+                        scalar1=gain[:, 0, h, j : j + 1],
+                        scalar2=shift[:, h, j : j + 1],
+                        op0=ALU.mult,
+                        op1=ALU.add,
+                    )
+                else:
+                    nc.scalar.activation(
+                        out=main_part[:, h, b, j, :],
+                        in_=by_channel[:, j, :],
+                        func=ACT.Identity,
+                        scale=gain[:, 0, h, j : j + 1],
+                        bias=shift[:, h, j : j + 1],
+                    )
 
-        def main_scale_and_shift(main_by_channel):
-            for n, (b, first) in enumerate(units):
-                for j in range(BLOCKS):
-                    row = first + j
-                    if n % 2 == 0:
-                        nc.vector.tensor_scalar(
-                            out=main_part[:, b, row, :],
-                            in0=main_by_channel[n][:, j, :],
-                            scalar1=gain[:, 0, row : row + 1],
-                            scalar2=shift[:, row : row + 1],
-                            op0=ALU.mult,
-                            op1=ALU.add,
-                        )
-                    else:
-                        nc.scalar.activation(
-                            out=main_part[:, b, row, :],
-                            in_=main_by_channel[n][:, j, :],
-                            func=ACT.Identity,
-                            scale=gain[:, 0, row : row + 1],
-                            bias=shift[:, row : row + 1],
-                        )
-
-        h_codes, h_scales = quantise(h_raw, BATCH, nc.scalar.copy)
-        quantise_chunk(0)
-        main_sum = main_passes(h_codes, h_scales)
-        for c in range(CHUNKS):
-            short_passes(c)
-            if c == 1:
-                main_by_channel = [transpose_blocks(main_by_position[b], first) for b, first in units]
-            if c + 1 < CHUNKS:
-                quantise_chunk(c + 1)
-            if c == 0:
-                main_by_position = [copy_out(main_sum[b]) for b in range(BATCH)]
-            if c == CHUNKS // 2:
-                main_scale_and_shift(main_by_channel)
-
-        short_by_position = [copy_out(short_sum[b]) for b in range(BATCH)]
-        for b, first in units:
-            by_channel = transpose_blocks(short_by_position[b], first)
+        def finish(h, b, by_channel):
             result = stage.tile([P, BLOCKS, POS], F32, tag="result")
             for j in range(BLOCKS):
-                row = first + j
                 nc.vector.scalar_tensor_tensor(
                     out=result[:, j, :],
                     in0=by_channel[:, j, :],
-                    scalar=gain[:, 1, row : row + 1],
-                    in1=main_part[:, b, row, :],
+                    scalar=gain[:, 1, h, j : j + 1],
+                    in1=main_part[:, h, b, j, :],
                     op0=ALU.mult,
                     op1=ALU.add,
                 )
             nc.scalar.activation(out=result[:], in_=result[:], func=ACT.Relu)
             nc.sync.dma_start(
-                out=out[b].rearrange("(p j) w -> p j w", j=PER_ROW)[:, first : first + BLOCKS, :], in_=result[:]
+                out=out[b, N_TILE * h : N_TILE * (h + 1), :].rearrange("(p j) w -> p j w", j=BLOCKS), in_=result[:]
             )
+
+        h_codes, h_scales = quantise(h_raw, BATCH, nc.scalar.copy)
+        quantise_chunk(0)
+        nc.vector.memset(sc_planes[1][:].bitcast(I32), 0)
+        load_rest()
+        main_sum = main_passes(h_codes, h_scales)
+        for c in range(LAST):
+            for b in range(BATCH):
+                for i in range(SIZES[c]):
+                    for h in range(HALVES):
+                        short_pass(c, b, i, h)
+            if c == 1:
+                main_by_channel = {u: transpose_blocks(main_by_position[u]) for u in units}
+            quantise_chunk(c + 1)
+            if c == 0:
+                main_by_position = {(h, b): copy_out(main_sum[(h, b)], b) for h, b in units}
+            if c == CHUNKS // 2:
+                for h, b in units:
+                    main_scale_and_shift(h, b, main_by_channel[(h, b)])
+
+        short_by_position = {}
+        short_by_channel = {}
+        for h, b in units:
+            if (h, b) == units[-1]:
+                for u in units[:BATCH]:
+                    short_by_channel[u] = transpose_blocks(short_by_position[u])
+            for i in range(SIZES[LAST]):
+                short_pass(LAST, b, i, h)
+            short_by_position[(h, b)] = copy_out(short_sum[b][h], b)
+        for u in units[BATCH:]:
+            short_by_channel[u] = transpose_blocks(short_by_position[u])
+        for h, b in units:
+            finish(h, b, short_by_channel[(h, b)])

@@ -27,15 +27,14 @@ N_TILE = 512
 HALVES = C_OUT // N_TILE
 BLOCKS = N_TILE // P
 GROUPS = C_IN // K_PASS
-SIZES = (2, 2, 4, 4, 4, 4, 4, 4, 2, 2)
-FIRSTS = (0, 2, 4, 8, 12, 16, 20, 24, 28, 30)
-CHUNKS = len(SIZES)
+CHUNK = 2
+CHUNKS = GROUPS // CHUNK
 LAST = CHUNKS - 1
 QUADRANTS = 4
 ROWS = 4
-PLANE_GROUPS = 16
+PLANE_GROUPS = 4
 PLANE_TILES = GROUPS // PLANE_GROUPS
-TRICKLE = 2
+AHEAD = 6
 
 FLOPS = 2 * BATCH * C_OUT * (C_IN + C_MID) * POS
 
@@ -70,12 +69,12 @@ def tile_bottleneck_transformer_pb_k_kernel(
         work = ctx.enter_context(tc.psum_pool(name="work", bufs=4))
 
         x_raw = [
-            [keep.tile([P, SIZES[c], PACK, POS], BF16, name="x_raw_%d_%d" % (c, b)) for b in range(BATCH)]
+            [keep.tile([P, CHUNK, PACK, POS], BF16, name="x_raw_%d_%d" % (c, b)) for b in range(BATCH)]
             for c in range(CHUNKS)
         ]
         sc_words = [
             [
-                keep.tile([P, SIZES[c], 2 * C_OUT // parts], U8, name="sc_words_%d_%d" % (c, i), align_bytes=64)
+                keep.tile([P, CHUNK, 2 * C_OUT // parts], U8, name="sc_words_%d_%d" % (c, i), align_bytes=64)
                 for i in range(parts)
             ]
             for c, parts in enumerate([1] * LAST + [HALVES])
@@ -91,13 +90,14 @@ def tile_bottleneck_transformer_pb_k_kernel(
         main_part = keep.tile([P, HALVES, BATCH, BLOCKS, POS], F32)
 
         nc.vector.memset(c3_plane[:].bitcast(I32), 0)
-        nc.vector.memset(sc_planes[0][:].bitcast(I32), 0)
+        for plane in sc_planes[: AHEAD * CHUNK // PLANE_GROUPS]:
+            nc.vector.memset(plane[:].bitcast(I32), 0)
 
+        make_identity(nc, ident[:])
         vectors = (bn3_v, scbn_v, bn3_g, scbn_g, bn3_m, scbn_m, bn3_b, scbn_b, sc_b)
         slots = keep.tile([P, len(vectors), HALVES, 2 * BLOCKS], BF16)
         for v, vec in enumerate(vectors):
             nc.gpsimd.dma_start(out=slots[:, v, :, 0:BLOCKS], in_=vec.rearrange("(h p j) -> p h j", h=HALVES, p=P))
-        make_identity(nc, ident[:])
         variance, weight, mean = [slots[:, 2 * i : 2 * i + 2, :, 0:BLOCKS] for i in range(3)]
         minus_half = keep.tile([P, 2, HALVES, BLOCKS], F32)
         nc.gpsimd.memset(minus_half[:], -0.5)
@@ -117,49 +117,42 @@ def tile_bottleneck_transformer_pb_k_kernel(
         sc_scales_i32 = sc_w_scales.bitcast(I32)
         sc_words_i32 = sc_w_words.bitcast(I32)
 
-        scale_rows = [(r, quadrant) for r in range(ROWS) for quadrant in (0, 2, 1, 3)]
-
-        def load_scale_rows(i, first, count):
-            for r, quadrant in scale_rows[first : first + count]:
-                partition = 32 * quadrant + r
-                q = ROWS * quadrant + r
+        def load_scale_rows(i):
+            groups = slice(PLANE_GROUPS * i, PLANE_GROUPS * (i + 1))
+            for r in range(ROWS):
                 nc.sync.dma_start(
-                    out=sc_planes[i][:].bitcast(I32)[partition : partition + 1, :, :],
-                    in_=sc_scales_i32[PLANE_GROUPS * i : PLANE_GROUPS * (i + 1), q : q + 1, :].rearrange(
-                        "g o n -> o g n"
-                    ),
+                    out=sc_planes[i][:].bitcast(I32)[r:P:32, :, :],
+                    in_=sc_scales_i32[groups].rearrange("g (q r) n -> r q g n", r=ROWS)[r],
                 )
 
         def load_x(c, b):
-            rows = x[b, K_PASS * FIRSTS[c] : K_PASS * (FIRSTS[c] + SIZES[c]), :]
+            rows = x[b, K_PASS * CHUNK * c : K_PASS * CHUNK * (c + 1), :]
             nc.sync.dma_start(out=x_raw[c][b][:], in_=rows.rearrange("(g p t) w -> p g t w", p=P, t=PACK))
 
         def load_words(c, i):
-            words = sc_words_i32[FIRSTS[c] : FIRSTS[c] + SIZES[c]].rearrange("g p n -> p g n")
+            words = sc_words_i32[CHUNK * c : CHUNK * (c + 1)].rearrange("g p n -> p g n")
             width = words.shape[2] // len(sc_words[c])
             nc.sync.dma_start(out=sc_words[c][i][:].bitcast(I32), in_=words[:, :, width * i : width * (i + 1)])
 
         nc.sync.dma_start(out=h_raw[:], in_=h_attn.rearrange("b (p t) w -> p b t w", t=PACK))
         nc.sync.dma_start(out=c3_words[:].bitcast(I32), in_=conv3_w_words[0].bitcast(I32))
-        for quadrant in range(QUADRANTS):
+        for r in range(ROWS):
             nc.sync.dma_start(
-                out=c3_plane[32 * quadrant : 32 * quadrant + ROWS, :].bitcast(I32),
-                in_=conv3_w_scales[0, ROWS * quadrant : ROWS * (quadrant + 1), :].bitcast(I32),
+                out=c3_plane[:].bitcast(I32)[r:P:32, :],
+                in_=conv3_w_scales[0].bitcast(I32).rearrange("(q r) n -> r q n", r=ROWS)[r],
             )
-        for b in range(BATCH):
-            load_x(0, b)
-        load_words(0, 0)
-        load_scale_rows(0, 0, len(scale_rows))
 
-        def load_rest():
-            large = [(load_x, 1, 0), (load_x, 1, 1)]
-            for c in range(1, CHUNKS):
-                if c < LAST:
-                    large += [(load_x, c + 1, 0), (load_x, c + 1, 1)]
-                large += [(load_words, c, i) for i in range(len(sc_words[c]))]
-            for n, (load, c, i) in enumerate(large):
-                load(c, i)
-                load_scale_rows(1, TRICKLE * n, TRICKLE)
+        def load_chunk(c):
+            if CHUNK * c % PLANE_GROUPS == 0:
+                load_scale_rows(CHUNK * c // PLANE_GROUPS)
+            for n in (c, LAST) if c == LAST - 1 else (c,) if c < LAST else ():
+                for b in reversed(range(BATCH)):
+                    load_x(n, b)
+            for i in range(len(sc_words[c])):
+                load_words(c, i)
+
+        for c in range(AHEAD):
+            load_chunk(c)
 
         def quantise(raw, blocks, copy):
             grouped = stage.tile([P, blocks, POS, PACK], BF16, tag="grouped", align_bytes=64)
@@ -174,8 +167,13 @@ def tile_bottleneck_transformer_pb_k_kernel(
         x_q = {}
 
         def quantise_chunk(c):
-            x_q[(c, 0)] = quantise(x_raw[c][0], SIZES[c], nc.vector.tensor_copy)
-            x_q[(c, 1)] = quantise(x_raw[c][1], SIZES[c], nc.scalar.copy)
+            x_q[(c, 0)] = quantise(x_raw[c][0], CHUNK, nc.vector.tensor_copy)
+            x_q[(c, 1)] = quantise(x_raw[c][1], CHUNK, nc.scalar.copy)
+            ahead = c + AHEAD
+            if ahead < CHUNKS:
+                if CHUNK * ahead % PLANE_GROUPS == 0:
+                    nc.vector.memset(sc_planes[CHUNK * ahead // PLANE_GROUPS][:].bitcast(I32), 0)
+                load_chunk(ahead)
 
         short_sum = [
             [sums.tile([P, N_TILE], F32, name="short_sum_%d_%d" % (b, h)) for h in range(HALVES)]
@@ -184,7 +182,7 @@ def tile_bottleneck_transformer_pb_k_kernel(
 
         def short_pass(c, b, i, h):
             codes, scales = x_q[(c, b)]
-            g = FIRSTS[c] + i
+            g = CHUNK * c + i
             words = sc_words[c]
             rhs = words[h][:, i, :] if len(words) > 1 else words[0][:, i, 2 * N_TILE * h : 2 * N_TILE * (h + 1)]
             nc.tensor.matmul_mx(
@@ -265,20 +263,18 @@ def tile_bottleneck_transformer_pb_k_kernel(
 
         h_codes, h_scales = quantise(h_raw, BATCH, nc.scalar.copy)
         quantise_chunk(0)
-        nc.vector.memset(sc_planes[1][:].bitcast(I32), 0)
-        load_rest()
         main_sum = main_passes(h_codes, h_scales)
         for c in range(LAST):
             for b in range(BATCH):
-                for i in range(SIZES[c]):
+                for i in range(CHUNK):
                     for h in range(HALVES):
                         short_pass(c, b, i, h)
-            if c == 1:
+            if c == 2:
                 main_by_channel = {u: transpose_blocks(main_by_position[u]) for u in units}
             quantise_chunk(c + 1)
             if c == 0:
                 main_by_position = {(h, b): copy_out(main_sum[(h, b)], b) for h, b in units}
-            if c == CHUNKS // 2:
+            if c == LAST // 2:
                 for h, b in units:
                     main_scale_and_shift(h, b, main_by_channel[(h, b)])
 
@@ -288,7 +284,7 @@ def tile_bottleneck_transformer_pb_k_kernel(
             if (h, b) == units[-1]:
                 for u in units[:BATCH]:
                     short_by_channel[u] = transpose_blocks(short_by_position[u])
-            for i in range(SIZES[LAST]):
+            for i in range(CHUNK):
                 short_pass(LAST, b, i, h)
             short_by_position[(h, b)] = copy_out(short_sum[b][h], b)
         for u in units[BATCH:]:

@@ -32,9 +32,11 @@ CHUNKS = GROUPS // CHUNK
 LAST = CHUNKS - 1
 QUADRANTS = 4
 ROWS = 4
-PLANE_GROUPS = 4
+PLANE_GROUPS = 16
 PLANE_TILES = GROUPS // PLANE_GROUPS
-AHEAD = 6
+AHEAD = 3
+SECOND_RUN = 5
+ZERO_STEPS = 4
 
 FLOPS = 2 * BATCH * C_OUT * (C_IN + C_MID) * POS
 
@@ -87,42 +89,63 @@ def tile_bottleneck_transformer_pb_k_kernel(
         c3_words = keep.tile([P, 2 * C_OUT], U8, align_bytes=64)
         c3_plane = keep.tile([P, C_OUT], U8, align_bytes=64)
         ident = keep.tile([P, P], F32)
+        ident_bf16 = keep.tile([P, P], BF16)
         main_part = keep.tile([P, HALVES, BATCH, BLOCKS, POS], F32)
 
         nc.vector.memset(c3_plane[:].bitcast(I32), 0)
-        for plane in sc_planes[: AHEAD * CHUNK // PLANE_GROUPS]:
-            nc.vector.memset(plane[:].bitcast(I32), 0)
+        nc.vector.memset(sc_planes[0][:].bitcast(I32), 0)
 
-        make_identity(nc, ident[:])
+        def zero_second_plane(step):
+            groups = PLANE_GROUPS // ZERO_STEPS
+            nc.vector.memset(sc_planes[1][:, groups * step : groups * (step + 1), :].bitcast(I32), 0)
+
         vectors = (bn3_v, scbn_v, bn3_g, scbn_g, bn3_m, scbn_m, bn3_b, scbn_b, sc_b)
-        slots = keep.tile([P, len(vectors), HALVES, 2 * BLOCKS], BF16)
+        rows = keep.tile([P, N_TILE], BF16)
+        nc.gpsimd.memset(rows[:], 0.0)
+        make_identity(nc, ident[:])
+        make_identity(nc, ident_bf16[:])
         for v, vec in enumerate(vectors):
-            nc.gpsimd.dma_start(out=slots[:, v, :, 0:BLOCKS], in_=vec.rearrange("(h p j) -> p h j", h=HALVES, p=P))
-        variance, weight, mean = [slots[:, 2 * i : 2 * i + 2, :, 0:BLOCKS] for i in range(3)]
-        minus_half = keep.tile([P, 2, HALVES, BLOCKS], F32)
-        nc.gpsimd.memset(minus_half[:], -0.5)
+            nc.gpsimd.dma_start(
+                out=rows[HALVES * v : HALVES * (v + 1), :], in_=vec.rearrange("(h n) -> h n", h=HALVES)
+            )
         gain = keep.tile([P, 2, HALVES, BLOCKS], F32)
-        nc.gpsimd.tensor_scalar_add(gain[:], variance, EPS)
-        nc.gpsimd.tensor_tensor(out=gain[:], in0=gain[:], in1=minus_half[:], op=ALU.pow)
-        nc.gpsimd.tensor_tensor(out=gain[:], in0=gain[:], in1=weight, op=ALU.mult)
-        mean_gain = keep.tile([P, 2, HALVES, BLOCKS], F32)
-        nc.gpsimd.tensor_tensor(out=mean_gain[:], in0=gain[:], in1=mean, op=ALU.mult)
         shift = keep.tile([P, HALVES, BLOCKS], F32)
-        nc.gpsimd.tensor_tensor(out=shift[:], in0=gain[:, 1], in1=slots[:, 8, :, 0:BLOCKS], op=ALU.mult)
-        nc.gpsimd.tensor_tensor(out=shift[:], in0=shift[:], in1=slots[:, 6, :, 0:BLOCKS], op=ALU.add)
-        nc.gpsimd.tensor_tensor(out=shift[:], in0=shift[:], in1=slots[:, 7, :, 0:BLOCKS], op=ALU.add)
-        nc.gpsimd.tensor_tensor(out=shift[:], in0=shift[:], in1=mean_gain[:, 0], op=ALU.subtract)
-        nc.gpsimd.tensor_tensor(out=shift[:], in0=shift[:], in1=mean_gain[:, 1], op=ALU.subtract)
+
+        def gains_and_shift():
+            turned = work.tile([P, BLOCKS, P], BF16, tag="work")
+            for j in range(BLOCKS):
+                nc.tensor.transpose(turned[:, j, :], rows[:, j:N_TILE:BLOCKS], ident_bf16[:])
+            columns = keep.tile([P, BLOCKS, len(vectors) * HALVES], F32)
+            nc.vector.tensor_copy(out=columns[:], in_=turned[:, :, 0 : len(vectors) * HALVES])
+            vec = columns[:].rearrange("p j (v h) -> p v h j", h=HALVES)
+            variance, weight, mean = [vec[:, 2 * i : 2 * i + 2] for i in range(3)]
+            minus_half = keep.tile([P, 2, HALVES, BLOCKS], F32)
+            nc.gpsimd.memset(minus_half[:], -0.5)
+            nc.gpsimd.tensor_scalar_add(gain[:], variance, EPS)
+            nc.gpsimd.tensor_tensor(out=gain[:], in0=gain[:], in1=minus_half[:], op=ALU.pow)
+            nc.gpsimd.tensor_tensor(out=gain[:], in0=gain[:], in1=weight, op=ALU.mult)
+            mean_gain = keep.tile([P, 2, HALVES, BLOCKS], F32)
+            nc.gpsimd.tensor_tensor(out=mean_gain[:], in0=gain[:], in1=mean, op=ALU.mult)
+            nc.gpsimd.tensor_tensor(out=shift[:], in0=gain[:, 1], in1=vec[:, 8], op=ALU.mult)
+            nc.gpsimd.tensor_tensor(out=shift[:], in0=shift[:], in1=vec[:, 6], op=ALU.add)
+            nc.gpsimd.tensor_tensor(out=shift[:], in0=shift[:], in1=vec[:, 7], op=ALU.add)
+            nc.gpsimd.tensor_tensor(out=shift[:], in0=shift[:], in1=mean_gain[:, 0], op=ALU.subtract)
+            nc.gpsimd.tensor_tensor(out=shift[:], in0=shift[:], in1=mean_gain[:, 1], op=ALU.subtract)
 
         sc_scales_i32 = sc_w_scales.bitcast(I32)
         sc_words_i32 = sc_w_words.bitcast(I32)
 
+        scale_rows = [(r, quadrant) for r in range(ROWS) for quadrant in (0, 2, 1, 3)]
+
         def load_scale_rows(i):
-            groups = slice(PLANE_GROUPS * i, PLANE_GROUPS * (i + 1))
-            for r in range(ROWS):
+            for r, quadrant in scale_rows:
+                partition = 32 * quadrant + r
+                q = ROWS * quadrant + r
                 nc.sync.dma_start(
-                    out=sc_planes[i][:].bitcast(I32)[r:P:32, :, :],
-                    in_=sc_scales_i32[groups].rearrange("g (q r) n -> r q g n", r=ROWS)[r],
+                    out=sc_planes[i][:].bitcast(I32)[partition : partition + 1, :, :],
+                    in_=sc_scales_i32[PLANE_GROUPS * i : PLANE_GROUPS * (i + 1), q : q + 1, :].rearrange(
+                        "g o n -> o g n"
+                    ),
                 )
 
         def load_x(c, b):
@@ -143,13 +166,15 @@ def tile_bottleneck_transformer_pb_k_kernel(
             )
 
         def load_chunk(c):
-            if CHUNK * c % PLANE_GROUPS == 0:
-                load_scale_rows(CHUNK * c // PLANE_GROUPS)
+            if c == SECOND_RUN:
+                load_scale_rows(1)
             for n in (c, LAST) if c == LAST - 1 else (c,) if c < LAST else ():
                 for b in reversed(range(BATCH)):
                     load_x(n, b)
             for i in range(len(sc_words[c])):
                 load_words(c, i)
+            if c == 0:
+                load_scale_rows(0)
 
         for c in range(AHEAD):
             load_chunk(c)
@@ -169,10 +194,11 @@ def tile_bottleneck_transformer_pb_k_kernel(
         def quantise_chunk(c):
             x_q[(c, 0)] = quantise(x_raw[c][0], CHUNK, nc.vector.tensor_copy)
             x_q[(c, 1)] = quantise(x_raw[c][1], CHUNK, nc.scalar.copy)
+            if c < 2:
+                zero_second_plane(2 * c)
+                zero_second_plane(2 * c + 1)
             ahead = c + AHEAD
             if ahead < CHUNKS:
-                if CHUNK * ahead % PLANE_GROUPS == 0:
-                    nc.vector.memset(sc_planes[CHUNK * ahead // PLANE_GROUPS][:].bitcast(I32), 0)
                 load_chunk(ahead)
 
         short_sum = [
@@ -269,7 +295,8 @@ def tile_bottleneck_transformer_pb_k_kernel(
                 for i in range(CHUNK):
                     for h in range(HALVES):
                         short_pass(c, b, i, h)
-            if c == 2:
+            if c == 3:
+                gains_and_shift()
                 main_by_channel = {u: transpose_blocks(main_by_position[u]) for u in units}
             quantise_chunk(c + 1)
             if c == 0:

@@ -26,17 +26,18 @@ EPS = 1e-5
 N_TILE = 512
 HALVES = C_OUT // N_TILE
 BLOCKS = N_TILE // P
+PAIR = BLOCKS // BATCH
 GROUPS = C_IN // K_PASS
 CHUNK = 2
 CHUNKS = GROUPS // CHUNK
 LAST = CHUNKS - 1
 QUADRANTS = 4
 ROWS = 4
-PLANE_GROUPS = 16
-PLANE_TILES = GROUPS // PLANE_GROUPS
-AHEAD = 3
-SECOND_RUN = 5
-ZERO_STEPS = 4
+PLANE_FIRSTS = (0, 8, 24)
+PLANE_GROUPS = (8, 16, 8)
+PLANES = len(PLANE_FIRSTS)
+WOVEN = ((1, 3, 2), (2, 14, 1))
+ZERO_GROUPS = 4
 
 FLOPS = 2 * BATCH * C_OUT * (C_IN + C_MID) * POS
 
@@ -82,22 +83,23 @@ def tile_bottleneck_transformer_pb_k_kernel(
             for c, parts in enumerate([1] * LAST + [HALVES])
         ]
         sc_planes = [
-            keep.tile([P, PLANE_GROUPS, C_OUT], U8, name="sc_planes_%d" % i, align_bytes=64)
-            for i in range(PLANE_TILES)
+            keep.tile([P, PLANE_GROUPS[i], C_OUT], U8, name="sc_planes_%d" % i, align_bytes=64)
+            for i in range(PLANES)
         ]
         h_raw = keep.tile([P, BATCH, PACK, POS], BF16)
         c3_words = keep.tile([P, 2 * C_OUT], U8, align_bytes=64)
         c3_plane = keep.tile([P, C_OUT], U8, align_bytes=64)
         ident = keep.tile([P, P], F32)
         ident_bf16 = keep.tile([P, P], BF16)
-        main_part = keep.tile([P, HALVES, BATCH, BLOCKS, POS], F32)
+        main_part = keep.tile([P, HALVES, BLOCKS, BATCH, POS], F32)
+
+        def zero_planes(i, first, count):
+            for group in range(first, first + count, ZERO_GROUPS):
+                nc.vector.memset(sc_planes[i][:, group : group + ZERO_GROUPS, :].bitcast(I32), 0)
 
         nc.vector.memset(c3_plane[:].bitcast(I32), 0)
-        nc.vector.memset(sc_planes[0][:].bitcast(I32), 0)
-
-        def zero_second_plane(step):
-            groups = PLANE_GROUPS // ZERO_STEPS
-            nc.vector.memset(sc_planes[1][:, groups * step : groups * (step + 1), :].bitcast(I32), 0)
+        zero_planes(0, 0, PLANE_GROUPS[0])
+        zero_planes(1, 0, PLANE_GROUPS[1] // 2)
 
         vectors = (bn3_v, scbn_v, bn3_g, scbn_g, bn3_m, scbn_m, bn3_b, scbn_b, sc_b)
         rows = keep.tile([P, N_TILE], BF16)
@@ -135,18 +137,24 @@ def tile_bottleneck_transformer_pb_k_kernel(
         sc_scales_i32 = sc_w_scales.bitcast(I32)
         sc_words_i32 = sc_w_words.bitcast(I32)
 
+        def load_first_scale_rows():
+            for r in range(ROWS):
+                nc.sync.dma_start(
+                    out=sc_planes[0][:].bitcast(I32)[r:P:32, :, :],
+                    in_=sc_scales_i32[: PLANE_GROUPS[0]].rearrange("g (q r) n -> r q g n", r=ROWS)[r],
+                )
+
         scale_rows = [(r, quadrant) for r in range(ROWS) for quadrant in (0, 2, 1, 3)]
 
-        def load_scale_rows(i):
-            for r, quadrant in scale_rows:
-                partition = 32 * quadrant + r
-                q = ROWS * quadrant + r
-                nc.sync.dma_start(
-                    out=sc_planes[i][:].bitcast(I32)[partition : partition + 1, :, :],
-                    in_=sc_scales_i32[PLANE_GROUPS * i : PLANE_GROUPS * (i + 1), q : q + 1, :].rearrange(
-                        "g o n -> o g n"
-                    ),
-                )
+        def load_scale_row(i, n):
+            r, quadrant = scale_rows[n]
+            partition = 32 * quadrant + r
+            q = ROWS * quadrant + r
+            groups = slice(PLANE_FIRSTS[i], PLANE_FIRSTS[i] + PLANE_GROUPS[i])
+            nc.sync.dma_start(
+                out=sc_planes[i][:].bitcast(I32)[partition : partition + 1, :, :],
+                in_=sc_scales_i32[groups, q : q + 1, :].rearrange("g o n -> o g n"),
+            )
 
         def load_x(c, b):
             rows = x[b, K_PASS * CHUNK * c : K_PASS * CHUNK * (c + 1), :]
@@ -166,18 +174,21 @@ def tile_bottleneck_transformer_pb_k_kernel(
             )
 
         def load_chunk(c):
-            if c == SECOND_RUN:
-                load_scale_rows(1)
+            large = []
             for n in (c, LAST) if c == LAST - 1 else (c,) if c < LAST else ():
-                for b in reversed(range(BATCH)):
-                    load_x(n, b)
-            for i in range(len(sc_words[c])):
-                load_words(c, i)
-            if c == 0:
-                load_scale_rows(0)
+                large += [(load_x, n, b) for b in reversed(range(BATCH))]
+            large += [(load_words, c, i) for i in range(len(sc_words[c]))]
+            for turn, (load, n, i) in enumerate(large, (BATCH + 1) * c):
+                if turn == BATCH:
+                    load_first_scale_rows()
+                load(n, i)
+                for plane, first, count in WOVEN:
+                    done = count * (turn - first)
+                    for row in range(done, done + count):
+                        if 0 <= row < len(scale_rows):
+                            load_scale_row(plane, row)
 
-        for c in range(AHEAD):
-            load_chunk(c)
+        load_chunk(0)
 
         def quantise(raw, blocks, copy):
             grouped = stage.tile([P, blocks, POS, PACK], BF16, tag="grouped", align_bytes=64)
@@ -194,12 +205,6 @@ def tile_bottleneck_transformer_pb_k_kernel(
         def quantise_chunk(c):
             x_q[(c, 0)] = quantise(x_raw[c][0], CHUNK, nc.vector.tensor_copy)
             x_q[(c, 1)] = quantise(x_raw[c][1], CHUNK, nc.scalar.copy)
-            if c < 2:
-                zero_second_plane(2 * c)
-                zero_second_plane(2 * c + 1)
-            ahead = c + AHEAD
-            if ahead < CHUNKS:
-                load_chunk(ahead)
 
         short_sum = [
             [sums.tile([P, N_TILE], F32, name="short_sum_%d_%d" % (b, h)) for h in range(HALVES)]
@@ -210,13 +215,14 @@ def tile_bottleneck_transformer_pb_k_kernel(
             codes, scales = x_q[(c, b)]
             g = CHUNK * c + i
             words = sc_words[c]
+            plane = max(n for n in range(PLANES) if PLANE_FIRSTS[n] <= g)
             rhs = words[h][:, i, :] if len(words) > 1 else words[0][:, i, 2 * N_TILE * h : 2 * N_TILE * (h + 1)]
             nc.tensor.matmul_mx(
                 out=short_sum[b][h][:],
                 lhsT=codes[:, POS * i : POS * (i + 1)].bitcast(FP8X4),
                 lhsT_scale=scales[:, POS * i : POS * (i + 1)],
                 rhs=rhs.bitcast(FP4X4),
-                rhs_scale=sc_planes[g // PLANE_GROUPS][:, g % PLANE_GROUPS, N_TILE * h : N_TILE * (h + 1)],
+                rhs_scale=sc_planes[plane][:, g - PLANE_FIRSTS[plane], N_TILE * h : N_TILE * (h + 1)],
                 start=(g == 0),
                 stop=(g == GROUPS - 1),
             )
@@ -245,50 +251,58 @@ def tile_bottleneck_transformer_pb_k_kernel(
             copy(out=by_position[:], in_=bank[:].rearrange("q (p j) -> q j p", j=BLOCKS))
             return by_position
 
-        def transpose_blocks(by_position):
-            by_channel = work.tile([P, BLOCKS, POS], F32, tag="work")
-            for j in range(BLOCKS):
-                nc.tensor.transpose(by_channel[:, j, :], by_position[:, j, :], ident[:])
+        blocks = [(h, j) for h in range(HALVES) for j in range(0, BLOCKS, PAIR)]
+
+        def transpose_blocks(h, first, by_position):
+            by_channel = work.tile([P, PAIR, BATCH, POS], F32, tag="work")
+            for j in range(PAIR):
+                for b in range(BATCH):
+                    nc.tensor.transpose(by_channel[:, j, b, :], by_position[(h, b)][:, first + j, :], ident[:])
             return by_channel
 
-        def main_scale_and_shift(h, b, by_channel):
-            for j in range(BLOCKS):
-                if b == 0:
+        def main_scale_and_shift(h, first, by_channel):
+            for j in range(PAIR):
+                row = first + j
+                if h == 0:
                     nc.vector.tensor_scalar(
-                        out=main_part[:, h, b, j, :],
-                        in0=by_channel[:, j, :],
-                        scalar1=gain[:, 0, h, j : j + 1],
-                        scalar2=shift[:, h, j : j + 1],
+                        out=main_part[:, h, row],
+                        in0=by_channel[:, j],
+                        scalar1=gain[:, 0, h, row : row + 1],
+                        scalar2=shift[:, h, row : row + 1],
                         op0=ALU.mult,
                         op1=ALU.add,
                     )
                 else:
                     nc.scalar.activation(
-                        out=main_part[:, h, b, j, :],
-                        in_=by_channel[:, j, :],
+                        out=main_part[:, h, row],
+                        in_=by_channel[:, j],
                         func=ACT.Identity,
-                        scale=gain[:, 0, h, j : j + 1],
-                        bias=shift[:, h, j : j + 1],
+                        scale=gain[:, 0, h, row : row + 1],
+                        bias=shift[:, h, row : row + 1],
                     )
 
-        def finish(h, b, by_channel):
-            result = stage.tile([P, BLOCKS, POS], F32, tag="result")
-            for j in range(BLOCKS):
+        def finish(h, first, by_channel, result):
+            for j in range(PAIR):
+                row = first + j
                 nc.vector.scalar_tensor_tensor(
-                    out=result[:, j, :],
-                    in0=by_channel[:, j, :],
-                    scalar=gain[:, 1, h, j : j + 1],
-                    in1=main_part[:, h, b, j, :],
+                    out=result[:, :, row, :],
+                    in0=by_channel[:, j],
+                    scalar=gain[:, 1, h, row : row + 1],
+                    in1=main_part[:, h, row],
                     op0=ALU.mult,
                     op1=ALU.add,
                 )
-            nc.scalar.activation(out=result[:], in_=result[:], func=ACT.Relu)
-            nc.sync.dma_start(
-                out=out[b, N_TILE * h : N_TILE * (h + 1), :].rearrange("(p j) w -> p j w", j=BLOCKS), in_=result[:]
-            )
+            pair = result[:, :, first : first + PAIR, :]
+            nc.scalar.activation(out=pair, in_=pair, func=ACT.Relu)
 
         h_codes, h_scales = quantise(h_raw, BATCH, nc.scalar.copy)
+        zero_planes(1, PLANE_GROUPS[1] // 2, PLANE_GROUPS[1] // 2)
+        for c in range(1, 4):
+            load_chunk(c)
         quantise_chunk(0)
+        zero_planes(2, 0, PLANE_GROUPS[2])
+        for c in range(4, CHUNKS):
+            load_chunk(c)
         main_sum = main_passes(h_codes, h_scales)
         for c in range(LAST):
             for b in range(BATCH):
@@ -297,24 +311,25 @@ def tile_bottleneck_transformer_pb_k_kernel(
                         short_pass(c, b, i, h)
             if c == 3:
                 gains_and_shift()
-                main_by_channel = {u: transpose_blocks(main_by_position[u]) for u in units}
+                main_by_channel = {u: transpose_blocks(*u, main_by_position) for u in blocks}
             quantise_chunk(c + 1)
             if c == 0:
                 main_by_position = {(h, b): copy_out(main_sum[(h, b)], b) for h, b in units}
             if c == LAST // 2:
-                for h, b in units:
-                    main_scale_and_shift(h, b, main_by_channel[(h, b)])
+                for u in blocks:
+                    main_scale_and_shift(*u, main_by_channel[u])
 
         short_by_position = {}
-        short_by_channel = {}
         for h, b in units:
-            if (h, b) == units[-1]:
-                for u in units[:BATCH]:
-                    short_by_channel[u] = transpose_blocks(short_by_position[u])
             for i in range(CHUNK):
                 short_pass(LAST, b, i, h)
             short_by_position[(h, b)] = copy_out(short_sum[b][h], b)
-        for u in units[BATCH:]:
-            short_by_channel[u] = transpose_blocks(short_by_position[u])
-        for h, b in units:
-            finish(h, b, short_by_channel[(h, b)])
+        for h in range(HALVES):
+            result = wide.tile([P, BATCH, BLOCKS, POS], F32, tag="result", bufs=HALVES)
+            for first in range(0, BLOCKS, PAIR):
+                finish(h, first, transpose_blocks(h, first, short_by_position), result)
+            for b in range(BATCH):
+                nc.sync.dma_start(
+                    out=out[b, N_TILE * h : N_TILE * (h + 1), :].rearrange("(p j) w -> p j w", j=BLOCKS),
+                    in_=result[:, b],
+                )

@@ -33,10 +33,10 @@ CHUNKS = GROUPS // CHUNK
 LAST = CHUNKS - 1
 QUADRANTS = 4
 ROWS = 4
-PLANE_FIRSTS = (0, 8, 24)
-PLANE_GROUPS = (8, 16, 8)
-PLANES = len(PLANE_FIRSTS)
-WOVEN = ((1, 3, 2), (2, 14, 1))
+PLANE_GROUPS = 16
+PLANES = GROUPS // PLANE_GROUPS
+BURSTS = (6, 6, 4)
+TRICKLE_FIRST = 6
 ZERO_GROUPS = 4
 
 FLOPS = 2 * BATCH * C_OUT * (C_IN + C_MID) * POS
@@ -77,18 +77,18 @@ def tile_bottleneck_transformer_pb_k_kernel(
         ]
         sc_words = [
             [
-                keep.tile([P, CHUNK, 2 * C_OUT // parts], U8, name="sc_words_%d_%d" % (c, i), align_bytes=64)
+                keep.tile([P, CHUNK, 2 * C_OUT // parts], U8, name="sc_words_%d_%d" % (c, i), align_bytes=256)
                 for i in range(parts)
             ]
             for c, parts in enumerate([1] * LAST + [HALVES])
         ]
         sc_planes = [
-            keep.tile([P, PLANE_GROUPS[i], C_OUT], U8, name="sc_planes_%d" % i, align_bytes=64)
+            keep.tile([P, PLANE_GROUPS, C_OUT], U8, name="sc_planes_%d" % i, align_bytes=256)
             for i in range(PLANES)
         ]
         h_raw = keep.tile([P, BATCH, PACK, POS], BF16)
-        c3_words = keep.tile([P, 2 * C_OUT], U8, align_bytes=64)
-        c3_plane = keep.tile([P, C_OUT], U8, align_bytes=64)
+        c3_words = keep.tile([P, 2 * C_OUT], U8, align_bytes=256)
+        c3_plane = keep.tile([P, C_OUT], U8, align_bytes=256)
         ident = keep.tile([P, P], F32)
         ident_bf16 = keep.tile([P, P], BF16)
         main_part = keep.tile([P, HALVES, BLOCKS, BATCH, POS], F32)
@@ -98,8 +98,7 @@ def tile_bottleneck_transformer_pb_k_kernel(
                 nc.vector.memset(sc_planes[i][:, group : group + ZERO_GROUPS, :].bitcast(I32), 0)
 
         nc.vector.memset(c3_plane[:].bitcast(I32), 0)
-        zero_planes(0, 0, PLANE_GROUPS[0])
-        zero_planes(1, 0, PLANE_GROUPS[1] // 2)
+        zero_planes(0, 0, PLANE_GROUPS)
 
         vectors = (bn3_v, scbn_v, bn3_g, scbn_g, bn3_m, scbn_m, bn3_b, scbn_b, sc_b)
         rows = keep.tile([P, N_TILE], BF16)
@@ -137,20 +136,13 @@ def tile_bottleneck_transformer_pb_k_kernel(
         sc_scales_i32 = sc_w_scales.bitcast(I32)
         sc_words_i32 = sc_w_words.bitcast(I32)
 
-        def load_first_scale_rows():
-            for r in range(ROWS):
-                nc.sync.dma_start(
-                    out=sc_planes[0][:].bitcast(I32)[r:P:32, :, :],
-                    in_=sc_scales_i32[: PLANE_GROUPS[0]].rearrange("g (q r) n -> r q g n", r=ROWS)[r],
-                )
-
         scale_rows = [(r, quadrant) for r in range(ROWS) for quadrant in (0, 2, 1, 3)]
 
         def load_scale_row(i, n):
             r, quadrant = scale_rows[n]
             partition = 32 * quadrant + r
             q = ROWS * quadrant + r
-            groups = slice(PLANE_FIRSTS[i], PLANE_FIRSTS[i] + PLANE_GROUPS[i])
+            groups = slice(PLANE_GROUPS * i, PLANE_GROUPS * (i + 1))
             nc.sync.dma_start(
                 out=sc_planes[i][:].bitcast(I32)[partition : partition + 1, :, :],
                 in_=sc_scales_i32[groups, q : q + 1, :].rearrange("g o n -> o g n"),
@@ -179,22 +171,23 @@ def tile_bottleneck_transformer_pb_k_kernel(
                 large += [(load_x, n, b) for b in reversed(range(BATCH))]
             large += [(load_words, c, i) for i in range(len(sc_words[c]))]
             for turn, (load, n, i) in enumerate(large, (BATCH + 1) * c):
-                if turn == BATCH:
-                    load_first_scale_rows()
                 load(n, i)
-                for plane, first, count in WOVEN:
-                    done = count * (turn - first)
-                    for row in range(done, done + count):
-                        if 0 <= row < len(scale_rows):
-                            load_scale_row(plane, row)
+                if turn < len(BURSTS):
+                    for row in range(sum(BURSTS[:turn]), sum(BURSTS[: turn + 1])):
+                        load_scale_row(0, row)
+                elif 0 <= turn - TRICKLE_FIRST < len(scale_rows):
+                    load_scale_row(1, turn - TRICKLE_FIRST)
 
         load_chunk(0)
 
-        def quantise(raw, blocks, copy):
-            grouped = stage.tile([P, blocks, POS, PACK], BF16, tag="grouped", align_bytes=64)
-            copy(out=grouped[:], in_=raw[:].rearrange("p g t w -> p g w t"))
-            codes = quant.tile([P, blocks * POS], U32, tag="codes", align_bytes=64)
-            scales = quant.tile([P, blocks * POS], U8, tag="scales", align_bytes=64)
+        def regroup(raw, blocks, copy):
+            grouped = stage.tile([P, blocks, POS, PACK], BF16, tag="grouped", align_bytes=256)
+            copy(out=grouped[:], in_=raw.rearrange("p g t w -> p g w t"))
+            return grouped
+
+        def quantise(grouped, blocks):
+            codes = quant.tile([P, blocks * POS], U32, tag="codes", align_bytes=256)
+            scales = quant.tile([P, blocks * POS], U8, tag="scales", align_bytes=256)
             nc.vector.quantize_mx(
                 out=codes[:].bitcast(FP8X4), scales=scales[:], in_=grouped[:].rearrange("p g w t -> p (g w t)")
             )
@@ -203,8 +196,11 @@ def tile_bottleneck_transformer_pb_k_kernel(
         x_q = {}
 
         def quantise_chunk(c):
-            x_q[(c, 0)] = quantise(x_raw[c][0], CHUNK, nc.vector.tensor_copy)
-            x_q[(c, 1)] = quantise(x_raw[c][1], CHUNK, nc.scalar.copy)
+            grouped = [
+                regroup(x_raw[c][b][:], CHUNK, copy) for b, copy in enumerate((nc.vector.tensor_copy, nc.scalar.copy))
+            ]
+            for b in reversed(range(BATCH)):
+                x_q[(c, b)] = quantise(grouped[b], CHUNK)
 
         short_sum = [
             [sums.tile([P, N_TILE], F32, name="short_sum_%d_%d" % (b, h)) for h in range(HALVES)]
@@ -215,14 +211,13 @@ def tile_bottleneck_transformer_pb_k_kernel(
             codes, scales = x_q[(c, b)]
             g = CHUNK * c + i
             words = sc_words[c]
-            plane = max(n for n in range(PLANES) if PLANE_FIRSTS[n] <= g)
             rhs = words[h][:, i, :] if len(words) > 1 else words[0][:, i, 2 * N_TILE * h : 2 * N_TILE * (h + 1)]
             nc.tensor.matmul_mx(
                 out=short_sum[b][h][:],
                 lhsT=codes[:, POS * i : POS * (i + 1)].bitcast(FP8X4),
                 lhsT_scale=scales[:, POS * i : POS * (i + 1)],
                 rhs=rhs.bitcast(FP4X4),
-                rhs_scale=sc_planes[plane][:, g - PLANE_FIRSTS[plane], N_TILE * h : N_TILE * (h + 1)],
+                rhs_scale=sc_planes[g // PLANE_GROUPS][:, g % PLANE_GROUPS, N_TILE * h : N_TILE * (h + 1)],
                 start=(g == 0),
                 stop=(g == GROUPS - 1),
             )
@@ -295,17 +290,16 @@ def tile_bottleneck_transformer_pb_k_kernel(
             pair = result[:, :, first : first + PAIR, :]
             nc.scalar.activation(out=pair, in_=pair, func=ACT.Relu)
 
-        h_codes, h_scales = quantise(h_raw, BATCH, nc.scalar.copy)
-        zero_planes(1, PLANE_GROUPS[1] // 2, PLANE_GROUPS[1] // 2)
-        for c in range(1, 4):
-            load_chunk(c)
+        h_codes, h_scales = quantise(regroup(h_raw[:], BATCH, nc.scalar.copy), BATCH)
+        zero_planes(1, 0, PLANE_GROUPS // 2)
+        load_chunk(1)
         quantise_chunk(0)
-        zero_planes(2, 0, PLANE_GROUPS[2])
-        for c in range(4, CHUNKS):
+        zero_planes(1, PLANE_GROUPS // 2, PLANE_GROUPS // 2)
+        for c in range(2, CHUNKS):
             load_chunk(c)
         main_sum = main_passes(h_codes, h_scales)
         for c in range(LAST):
-            for b in range(BATCH):
+            for b in reversed(range(BATCH)):
                 for i in range(CHUNK):
                     for h in range(HALVES):
                         short_pass(c, b, i, h)

from contextlib import ExitStack

import concourse.mybir as mybir
from concourse.masks import make_identity

F32 = mybir.dt.float32
BF16 = mybir.dt.bfloat16
I32 = mybir.dt.int32
U32 = mybir.dt.uint32
U8 = mybir.dt.uint8
FP8X4 = mybir.dt.float8_e4m3fn_x4
FP4X4 = mybir.dt.float4_e2m1fn_x4
ALU = mybir.AluOpType
ACT = mybir.ActivationFunctionType

P = 128
PACK = 4
K_PASS = P * PACK
BATCH = 2
POS = 128
C_MID = 512
C_IN = 16384
C_OUT = 1024
EPS = 1e-5

N_TILE = 512
HALVES = C_OUT // N_TILE
BLOCKS = N_TILE // P
PAIR = BLOCKS // BATCH
GROUPS = C_IN // K_PASS
CHUNK = 2
CHUNKS = GROUPS // CHUNK
LAST = CHUNKS - 1
QUADRANTS = 4
ROWS = 4
PLANE_GROUPS = 16
PLANES = GROUPS // PLANE_GROUPS
BURSTS = (6, 6, 4)
TRICKLE_FIRST = 6
ZERO_GROUPS = 4

FLOPS = 2 * BATCH * C_OUT * (C_IN + C_MID) * POS


def tile_bottleneck_transformer_pb_k_kernel(
    tc,
    h_attn,
    x,
    conv3_w_words,
    conv3_w_scales,
    bn3_g,
    bn3_b,
    bn3_m,
    bn3_v,
    sc_w_words,
    sc_w_scales,
    sc_b,
    scbn_g,
    scbn_b,
    scbn_m,
    scbn_v,
    out,
):
    nc = tc.nc
    with ExitStack() as ctx:
        ctx.enter_context(tc.manual_schedule())
        keep = ctx.enter_context(tc.tile_pool(name="keep", bufs=1))
        stage = ctx.enter_context(tc.tile_pool(name="stage", bufs=4))
        wide = ctx.enter_context(tc.tile_pool(name="wide", bufs=4))
        quant = ctx.enter_context(tc.tile_pool(name="quant", bufs=3 * BATCH + 1))
        sums = ctx.enter_context(tc.psum_pool(name="sums", bufs=1))
        work = ctx.enter_context(tc.psum_pool(name="work", bufs=4))

        x_raw = [
            [keep.tile([P, CHUNK, PACK, POS], BF16, name="x_raw_%d_%d" % (c, b)) for b in range(BATCH)]
            for c in range(CHUNKS)
        ]
        sc_words = [
            [
                keep.tile([P, CHUNK, 2 * C_OUT // parts], U8, name="sc_words_%d_%d" % (c, i), align_bytes=256)
                for i in range(parts)
            ]
            for c, parts in enumerate([1] * LAST + [HALVES])
        ]
        sc_planes = [
            keep.tile([P, PLANE_GROUPS, C_OUT], U8, name="sc_planes_%d" % i, align_bytes=256)
            for i in range(PLANES)
        ]
        h_raw = keep.tile([P, BATCH, PACK, POS], BF16)
        c3_words = keep.tile([P, 2 * C_OUT], U8, align_bytes=256)
        c3_plane = keep.tile([P, C_OUT], U8, align_bytes=256)
        ident = keep.tile([P, P], F32)
        ident_bf16 = keep.tile([P, P], BF16)
        main_part = keep.tile([P, HALVES, BLOCKS, BATCH, POS], F32)

        def zero_planes(i, first, count):
            for group in range(first, first + count, ZERO_GROUPS):
                nc.vector.memset(sc_planes[i][:, group : group + ZERO_GROUPS, :].bitcast(I32), 0)

        nc.vector.memset(c3_plane[:].bitcast(I32), 0)
        zero_planes(0, 0, PLANE_GROUPS)

        vectors = (bn3_v, scbn_v, bn3_g, scbn_g, bn3_m, scbn_m, bn3_b, scbn_b, sc_b)
        rows = keep.tile([P, N_TILE], BF16)
        nc.gpsimd.memset(rows[:], 0.0)
        make_identity(nc, ident[:])
        make_identity(nc, ident_bf16[:])
        for v, vec in enumerate(vectors):
            nc.gpsimd.dma_start(
                out=rows[HALVES * v : HALVES * (v + 1), :], in_=vec.rearrange("(h n) -> h n", h=HALVES)
            )
        gain = keep.tile([P, 2, HALVES, BLOCKS], F32)
        shift = keep.tile([P, HALVES, BLOCKS], F32)

        def gains_and_shift():
            turned = work.tile([P, BLOCKS, P], BF16, tag="work")
            for j in range(BLOCKS):
                nc.tensor.transpose(turned[:, j, :], rows[:, j:N_TILE:BLOCKS], ident_bf16[:])
            columns = keep.tile([P, BLOCKS, len(vectors) * HALVES], F32)
            nc.vector.tensor_copy(out=columns[:], in_=turned[:, :, 0 : len(vectors) * HALVES])
            vec = columns[:].rearrange("p j (v h) -> p v h j", h=HALVES)
            variance, weight, mean = [vec[:, 2 * i : 2 * i + 2] for i in range(3)]
            minus_half = keep.tile([P, 2, HALVES, BLOCKS], F32)
            nc.gpsimd.memset(minus_half[:], -0.5)
            nc.gpsimd.tensor_scalar_add(gain[:], variance, EPS)
            nc.gpsimd.tensor_tensor(out=gain[:], in0=gain[:], in1=minus_half[:], op=ALU.pow)
            nc.gpsimd.tensor_tensor(out=gain[:], in0=gain[:], in1=weight, op=ALU.mult)
            mean_gain = keep.tile([P, 2, HALVES, BLOCKS], F32)
            nc.gpsimd.tensor_tensor(out=mean_gain[:], in0=gain[:], in1=mean, op=ALU.mult)
            nc.gpsimd.tensor_tensor(out=shift[:], in0=gain[:, 1], in1=vec[:, 8], op=ALU.mult)
            nc.gpsimd.tensor_tensor(out=shift[:], in0=shift[:], in1=vec[:, 6], op=ALU.add)
            nc.gpsimd.tensor_tensor(out=shift[:], in0=shift[:], in1=vec[:, 7], op=ALU.add)
            nc.gpsimd.tensor_tensor(out=shift[:], in0=shift[:], in1=mean_gain[:, 0], op=ALU.subtract)
            nc.gpsimd.tensor_tensor(out=shift[:], in0=shift[:], in1=mean_gain[:, 1], op=ALU.subtract)

        sc_scales_i32 = sc_w_scales.bitcast(I32)
        sc_words_i32 = sc_w_words.bitcast(I32)

        scale_rows = [(r, quadrant) for r in range(ROWS) for quadrant in (0, 2, 1, 3)]

        def load_scale_row(i, n):
            r, quadrant = scale_rows[n]
            partition = 32 * quadrant + r
            q = ROWS * quadrant + r
            groups = slice(PLANE_GROUPS * i, PLANE_GROUPS * (i + 1))
            nc.sync.dma_start(
                out=sc_planes[i][:].bitcast(I32)[partition : partition + 1, :, :],
                in_=sc_scales_i32[groups, q : q + 1, :].rearrange("g o n -> o g n"),
            )

        def load_x(c, b):
            rows = x[b, K_PASS * CHUNK * c : K_PASS * CHUNK * (c + 1), :]
            nc.sync.dma_start(out=x_raw[c][b][:], in_=rows.rearrange("(g p t) w -> p g t w", p=P, t=PACK))

        def load_words(c, i):
            words = sc_words_i32[CHUNK * c : CHUNK * (c + 1)].rearrange("g p n -> p g n")
            width = words.shape[2] // len(sc_words[c])
            nc.sync.dma_start(out=sc_words[c][i][:].bitcast(I32), in_=words[:, :, width * i : width * (i + 1)])

        nc.sync.dma_start(out=h_raw[:], in_=h_attn.rearrange("b (p t) w -> p b t w", t=PACK))
        nc.sync.dma_start(out=c3_words[:].bitcast(I32), in_=conv3_w_words[0].bitcast(I32))
        for r in range(ROWS):
            nc.sync.dma_start(
                out=c3_plane[:].bitcast(I32)[r:P:32, :],
                in_=conv3_w_scales[0].bitcast(I32).rearrange("(q r) n -> r q n", r=ROWS)[r],
            )

        def load_chunk(c):
            large = []
            for n in (c, LAST) if c == LAST - 1 else (c,) if c < LAST else ():
                large += [(load_x, n, b) for b in reversed(range(BATCH))]
            large += [(load_words, c, i) for i in range(len(sc_words[c]))]
            for turn, (load, n, i) in enumerate(large, (BATCH + 1) * c):
                load(n, i)
                if turn < len(BURSTS):
                    for row in range(sum(BURSTS[:turn]), sum(BURSTS[: turn + 1])):
                        load_scale_row(0, row)
                elif 0 <= turn - TRICKLE_FIRST < len(scale_rows):
                    load_scale_row(1, turn - TRICKLE_FIRST)

        load_chunk(0)

        def regroup(raw, blocks, copy):
            grouped = stage.tile([P, blocks, POS, PACK], BF16, tag="grouped", align_bytes=256)
            copy(out=grouped[:], in_=raw.rearrange("p g t w -> p g w t"))
            return grouped

        def quantise(grouped, blocks):
            codes = quant.tile([P, blocks * POS], U32, tag="codes", align_bytes=256)
            scales = quant.tile([P, blocks * POS], U8, tag="scales", align_bytes=256)
            nc.vector.quantize_mx(
                out=codes[:].bitcast(FP8X4), scales=scales[:], in_=grouped[:].rearrange("p g w t -> p (g w t)")
            )
            return codes, scales

        x_q = {}

        def quantise_chunk(c):
            grouped = [
                regroup(x_raw[c][b][:], CHUNK, copy) for b, copy in enumerate((nc.vector.tensor_copy, nc.scalar.copy))
            ]
            for b in reversed(range(BATCH)):
                x_q[(c, b)] = quantise(grouped[b], CHUNK)

        short_sum = [
            [sums.tile([P, N_TILE], F32, name="short_sum_%d_%d" % (b, h)) for h in range(HALVES)]
            for b in range(BATCH)
        ]

        def short_pass(c, b, i, h):
            codes, scales = x_q[(c, b)]
            g = CHUNK * c + i
            words = sc_words[c]
            rhs = words[h][:, i, :] if len(words) > 1 else words[0][:, i, 2 * N_TILE * h : 2 * N_TILE * (h + 1)]
            nc.tensor.matmul_mx(
                out=short_sum[b][h][:],
                lhsT=codes[:, POS * i : POS * (i + 1)].bitcast(FP8X4),
                lhsT_scale=scales[:, POS * i : POS * (i + 1)],
                rhs=rhs.bitcast(FP4X4),
                rhs_scale=sc_planes[g // PLANE_GROUPS][:, g % PLANE_GROUPS, N_TILE * h : N_TILE * (h + 1)],
                start=(g == 0),
                stop=(g == GROUPS - 1),
            )

        def main_passes(codes, scales):
            main_sum = {}
            for b in range(BATCH):
                for h in range(HALVES):
                    main_sum[(h, b)] = work.tile([P, N_TILE], F32, tag="work", name="main_sum")
                    nc.tensor.matmul_mx(
                        out=main_sum[(h, b)][:],
                        lhsT=codes[:, POS * b : POS * (b + 1)].bitcast(FP8X4),
                        lhsT_scale=scales[:, POS * b : POS * (b + 1)],
                        rhs=c3_words[:, 2 * N_TILE * h : 2 * N_TILE * (h + 1)].bitcast(FP4X4),
                        rhs_scale=c3_plane[:, N_TILE * h : N_TILE * (h + 1)],
                        start=True,
                        stop=True,
                    )
            return main_sum

        units = [(h, b) for h in range(HALVES) for b in range(BATCH)]

        def copy_out(bank, b):
            by_position = wide.tile([P, BLOCKS, P], F32, tag="by_position")
            copy = nc.vector.tensor_copy if b == 0 else nc.scalar.copy
            copy(out=by_position[:], in_=bank[:].rearrange("q (p j) -> q j p", j=BLOCKS))
            return by_position

        blocks = [(h, j) for h in range(HALVES) for j in range(0, BLOCKS, PAIR)]

        def transpose_blocks(h, first, by_position):
            by_channel = work.tile([P, PAIR, BATCH, POS], F32, tag="work")
            for j in range(PAIR):
                for b in range(BATCH):
                    nc.tensor.transpose(by_channel[:, j, b, :], by_position[(h, b)][:, first + j, :], ident[:])
            return by_channel

        def main_scale_and_shift(h, first, by_channel):
            for j in range(PAIR):
                row = first + j
                if h == 0:
                    nc.vector.tensor_scalar(
                        out=main_part[:, h, row],
                        in0=by_channel[:, j],
                        scalar1=gain[:, 0, h, row : row + 1],
                        scalar2=shift[:, h, row : row + 1],
                        op0=ALU.mult,
                        op1=ALU.add,
                    )
                else:
                    nc.scalar.activation(
                        out=main_part[:, h, row],
                        in_=by_channel[:, j],
                        func=ACT.Identity,
                        scale=gain[:, 0, h, row : row + 1],
                        bias=shift[:, h, row : row + 1],
                    )

        def finish(h, first, by_channel, result):
            for j in range(PAIR):
                row = first + j
                nc.vector.scalar_tensor_tensor(
                    out=result[:, :, row, :],
                    in0=by_channel[:, j],
                    scalar=gain[:, 1, h, row : row + 1],
                    in1=main_part[:, h, row],
                    op0=ALU.mult,
                    op1=ALU.add,
                )
            pair = result[:, :, first : first + PAIR, :]
            nc.scalar.activation(out=pair, in_=pair, func=ACT.Relu)

        h_codes, h_scales = quantise(regroup(h_raw[:], BATCH, nc.scalar.copy), BATCH)
        zero_planes(1, 0, PLANE_GROUPS // 2)
        load_chunk(1)
        quantise_chunk(0)
        zero_planes(1, PLANE_GROUPS // 2, PLANE_GROUPS // 2)
        for c in range(2, CHUNKS):
            load_chunk(c)
        main_sum = main_passes(h_codes, h_scales)
        for c in range(LAST):
            for b in reversed(range(BATCH)):
                for i in range(CHUNK):
                    for h in range(HALVES):
                        short_pass(c, b, i, h)
            if c == 3:
                gains_and_shift()
                main_by_channel = {u: transpose_blocks(*u, main_by_position) for u in blocks}
            quantise_chunk(c + 1)
            if c == 0:
                main_by_position = {(h, b): copy_out(main_sum[(h, b)], b) for h, b in units}
            if c == LAST // 2:
                for u in blocks:
                    main_scale_and_shift(*u, main_by_channel[u])

        short_by_position = {}
        for h, b in units:
            for i in range(CHUNK):
                short_pass(LAST, b, i, h)
            short_by_position[(h, b)] = copy_out(short_sum[b][h], b)
        for h in range(HALVES):
            result = wide.tile([P, BATCH, BLOCKS, POS], F32, tag="result", bufs=HALVES)
            for first in range(0, BLOCKS, PAIR):
                finish(h, first, transpose_blocks(h, first, short_by_position), result)
            for b in range(BATCH):
                nc.sync.dma_start(
                    out=out[b, N_TILE * h : N_TILE * (h + 1), :].rearrange("(p j) w -> p j w", j=BLOCKS),
                    in_=result[:, b],
                )
